import numpy as np
import ml_dtypes


def mxq(x, axis, fmt="e4m3"):
    dtype, down = {"e4m3": (ml_dtypes.float8_e4m3fn, 7), "e5m2": (ml_dtypes.float8_e5m2, 14)}[fmt]
    v = np.moveaxis(np.asarray(x, np.float32).astype(ml_dtypes.bfloat16).astype(np.float64), axis, -1)
    blocks = v.reshape(v.shape[:-1] + (-1, 32))
    amax = np.abs(blocks).max(-1, keepdims=True)
    byte = np.maximum(np.where(amax > 0, np.frexp(amax)[1] - 1 + 127, 0) - down, 1)
    scale = np.exp2(byte - 127.0)
    codes = (blocks / scale).astype(np.float32).astype(dtype).astype(np.float64)
    return np.moveaxis((codes * scale).reshape(v.shape), -1, axis)


WIDE = False


def mx_kscale(k):
    if not WIDE:
        return np.ones(k)
    levels = np.array([10, -10, 5, -5, 0])
    a = np.random.permutation(np.resize(levels, k // 512 * 4)).reshape(k // 512, 4)
    idx = np.arange(k)
    return np.exp2(a[idx // 512, idx % 128 // 32])


BF16 = ml_dtypes.bfloat16


def bf(x):
    return np.asarray(x, np.float32).astype(BF16)


def f64(x):
    return np.asarray(x).astype(np.float64)


B, H, KVH, N, D, QB = 1, 4, 2, 512, 128, 512
MASK_VALUE = -float(np.finfo(np.float32).max)
QC = 4.0
BLK = 32


def setup_inputs():
    s = np.array(mx_kscale(N), dtype=np.float64)
    s[:BLK] = s.max()
    q = np.random.standard_normal((B, H, N, D)) * 1.5
    k = np.random.standard_normal((B, KVH, N, D)) * 1.5
    v = np.random.standard_normal((B, KVH, N, D))
    q[..., 0] = QC
    k[..., 0] += np.log2(s) * np.log(2.0) * np.sqrt(D) / QC
    v *= (s.max() / s)[:, None]
    return {"q": bf(q), "k": bf(k), "v": bf(v)}


def rep(a):
    return np.reshape(np.broadcast_to(a[:, None], (B, H // KVH, KVH, N, D)), (B, H, N, D))


def reference(q, k, v):
    q = f64(q)
    k = rep(f64(k))
    vq = rep(mxq(f64(v), 2, "e4m3"))
    outs = []
    for g in range(N // QB):
        lo, hi = g * QB, (g + 1) * QB
        s = q[:, :, lo:hi] @ k[:, :, :hi].transpose(0, 1, 3, 2) * (1.0 / np.sqrt(D))
        mask = np.arange(hi)[None, :] > np.arange(lo, hi)[:, None]
        s = np.where(mask, MASK_VALUE, s)
        e = np.exp(s - s.max(-1, keepdims=True))
        outs.append((mxq(e, 3, "e4m3") @ vq[:, :, :hi]) / e.sum(-1, keepdims=True))
    return np.concatenate(outs, axis=2)

@@ -1,0 +1,202 @@
+from contextlib import ExitStack
+
+import concourse.mybir as mybir
+from concourse.masks import make_identity
+
+F32 = mybir.dt.float32
+BF16 = mybir.dt.bfloat16
+U32 = mybir.dt.uint32
+U8 = mybir.dt.uint8
+FP8X4 = mybir.dt.float8_e4m3fn_x4
+ALU = mybir.AluOpType
+ACT = mybir.ActivationFunctionType
+AXIS = mybir.AxisListType
+
+P = 128
+H, KVH, N, D = 4, 2, 512, 128
+QT = N // P
+PACK = 4
+PAIRS = PACK // 2
+PAIR_COLS = N // PAIRS
+STEP = P // PAIRS
+SCALE = D ** -0.5
+MASKED = -(2.0 ** 127)
+
+FLOPS = 2 * 2 * H * N * N * D
+
+
+def tile_attend_s_kernel(tc, q, k, v, out):
+    nc = tc.nc
+    with ExitStack() as ctx:
+        keep = ctx.enter_context(tc.tile_pool(name="keep", bufs=1))
+        score_banks = ctx.enter_context(tc.psum_pool(name="score_banks", bufs=4))
+        turn_banks = ctx.enter_context(tc.psum_pool(name="turn_banks", bufs=2))
+        out_banks = ctx.enter_context(tc.psum_pool(name="out_banks", bufs=2))
+
+        k_rows = keep.tile([P, KVH, PACK, D], BF16)
+        v_rows = keep.tile([P, KVH, PACK, D], BF16)
+        q_rows = keep.tile([P, H, QT, D], BF16)
+
+        def load_keys(rows, src, g):
+            nc.sync.dma_start(out=rows[:, g], in_=src[0, g].rearrange("(p t) d -> p t d", t=PACK))
+
+        def load_queries(h):
+            nc.sync.dma_start(out=q_rows[:, h], in_=q[0, h].rearrange("(i r) d -> r i d", r=P))
+
+        load_keys(k_rows, k, 0)
+        load_queries(0)
+        load_keys(k_rows, k, 1)
+        load_queries(1)
+        load_keys(v_rows, v, 0)
+        load_keys(v_rows, v, 1)
+        load_queries(2)
+        load_queries(3)
+
+        ident_bf = keep.tile([P, P], BF16)
+        make_identity(nc, ident_bf[:])
+        ident_f32 = keep.tile([P, P], F32)
+        make_identity(nc, ident_f32[:])
+        causal = keep.tile([P, P], F32)
+        nc.gpsimd.memset(causal[:], 0.0)
+        nc.gpsimd.affine_select(
+            out=causal[:],
+            in_=causal[:],
+            compare_op=ALU.is_ge,
+            fill=MASKED,
+            base=0,
+            pattern=[[-1, P]],
+            channel_multiplier=1,
+        )
+        causal_bf = keep.tile([P, PAIRS, STEP], BF16)
+        nc.vector.tensor_copy(
+            out=causal_bf[:].rearrange("r u (p e) -> r u p e", e=2),
+            in_=causal[:].rearrange("r (p u e) -> r u p e", u=PAIRS, e=2),
+        )
+        warm = keep.tile([P, 1], F32)
+        nc.vector.memset(warm[:], 0.0)
+        nc.scalar.activation(out=warm[:], in_=warm[:], func=ACT.Exp)
+
+        kT = keep.tile([P, KVH, PAIRS, PAIR_COLS], BF16)
+        qT = keep.tile([P, H, QT, P], BF16)
+        e_all = keep.tile([P, H, QT, PAIRS, PAIR_COLS], BF16)
+        row_max = keep.tile([P, H, QT], F32)
+        shift = keep.tile([P, H, QT], F32)
+        row_sum = keep.tile([P, H, QT], F32)
+        inv_sum = keep.tile([P, H, QT], F32)
+        e_grouped = keep.tile([P, H, QT, P, PACK], BF16, align_bytes=64)
+        e_codes = keep.tile([P, H, QT, P], U32, align_bytes=64)
+        e_scales = keep.tile([P, H, QT, P], U8, align_bytes=64)
+        v_grouped = keep.tile([P, KVH, D, PACK], BF16, align_bytes=64)
+        v_codes = keep.tile([P, KVH, D], U32, align_bytes=64)
+        v_scales = keep.tile([P, KVH, D], U8, align_bytes=64)
+        o_all = keep.tile([P, H, QT, D], F32)
+
+        for i in range(QT - 1):
+            nc.vector.memset(e_all[:, :, i, :, STEP * (i + 1) :], 0.0)
+
+        def turn_keys(g):
+            kt_ps = turn_banks.tile([P, PACK, P], BF16, tag="turn")
+            for t in range(PACK):
+                nc.tensor.transpose(kt_ps[:, t, :], k_rows[:, g, t, :], ident_bf[:])
+            nc.vector.tensor_copy(
+                out=kT[:, g].rearrange("d u (p e) -> d u p e", e=2),
+                in_=kt_ps[:].rearrange("d (u e) p -> d u p e", e=2),
+            )
+
+        def turn_queries(h):
+            qt_ps = turn_banks.tile([P, QT, P], BF16, tag="turn")
+            for i in range(QT):
+                nc.tensor.transpose(qt_ps[:, i, :], q_rows[:, h, i, :], ident_bf[:])
+            nc.scalar.copy(out=qT[:, h], in_=qt_ps[:])
+
+        def quantise_values():
+            nc.vector.tensor_copy(out=v_grouped[:], in_=v_rows[:].rearrange("p g t d -> p g d t"))
+            nc.vector.quantize_mx(
+                out=v_codes[:].rearrange("p g d -> p (g d)").bitcast(FP8X4),
+                scales=v_scales[:].rearrange("p g d -> p (g d)"),
+                in_=v_grouped[:].rearrange("p g d t -> p (g d t)"),
+            )
+
+        def softmax_numerators(h, i):
+            cols = STEP * (i + 1)
+            s_ps = score_banks.tile([P, PAIRS, cols], F32, tag="s")
+            seen = STEP * i
+            nc.tensor.matmul(
+                out=s_ps[:, :, seen:], lhsT=ident_bf[:], rhs=causal_bf[:], start=True, stop=False
+            )
+            nc.tensor.matmul(
+                out=s_ps[:, :, seen:],
+                lhsT=qT[:, h, i, :],
+                rhs=kT[:, h % KVH, :, seen:cols],
+                start=False,
+                stop=True,
+            )
+            if seen > 0:
+                nc.tensor.matmul(
+                    out=s_ps[:, :, :seen],
+                    lhsT=qT[:, h, i, :],
+                    rhs=kT[:, h % KVH, :, :seen],
+                    start=True,
+                    stop=True,
+                )
+            nc.vector.reduce_max(out=row_max[:, h, i : i + 1], in_=s_ps[:], axis=AXIS.XY)
+            nc.scalar.mul(out=shift[:, h, i : i + 1], in_=row_max[:, h, i : i + 1], mul=-SCALE)
+            nc.scalar.activation(
+                out=e_all[:, h, i, :, :cols],
+                in_=s_ps[:],
+                func=ACT.Exp,
+                bias=shift[:, h, i : i + 1],
+                scale=SCALE,
+                accum_out=row_sum[:, h, i : i + 1],
+            )
+
+        def attend(h, first):
+            two = slice(first, first + 2)
+            e_words = e_all[:, h, two].bitcast(F32)
+            et_ps = turn_banks.tile([P, 2, PAIRS, P], F32, tag="turn")
+            for a in range(2):
+                for u in range(PAIRS):
+                    nc.tensor.transpose(et_ps[:, a, u, :], e_words[:, a, u, :], ident_f32[:])
+            nc.scalar.copy(
+                out=e_grouped[:, h, two].bitcast(F32), in_=et_ps[:].rearrange("p a u r -> p a r u")
+            )
+            nc.vector.quantize_mx(
+                out=e_codes[:, h, two].rearrange("p a r -> p (a r)").bitcast(FP8X4),
+                scales=e_scales[:, h, two].rearrange("p a r -> p (a r)"),
+                in_=e_grouped[:, h, two].rearrange("p a r t -> p (a r t)"),
+            )
+            o_ps = out_banks.tile([P, 2, D], F32, tag="o")
+            for a in range(2):
+                i = first + a
+                nc.tensor.matmul_mx(
+                    out=o_ps[:, a, :],
+                    lhsT=e_codes[:, h, i, :].bitcast(FP8X4),
+                    lhsT_scale=e_scales[:, h, i, :],
+                    rhs=v_codes[:, h % KVH, :].bitcast(FP8X4),
+                    rhs_scale=v_scales[:, h % KVH, :],
+                    start=True,
+                    stop=True,
+                )
+            nc.vector.reciprocal(out=inv_sum[:, h, two], in_=row_sum[:, h, two])
+            nc.vector.tensor_tensor(
+                out=o_all[:, h, two, :],
+                in0=o_ps[:],
+                in1=inv_sum[:, h, two].unsqueeze(2).to_broadcast([P, 2, D]),
+                op=ALU.mult,
+            )
+            nc.sync.dma_start(
+                out=out[0, h].rearrange("(i r) d -> r i d", r=P)[:, two, :], in_=o_all[:, h, two, :]
+            )
+
+        turn_keys(0)
+        turn_queries(0)
+        turn_keys(1)
+        turn_queries(1)
+        quantise_values()
+        turn_queries(2)
+        turn_queries(3)
+        for h in range(H):
+            for first in range(0, QT, 2):
+                softmax_numerators(h, first)
+                softmax_numerators(h, first + 1)
+                attend(h, first)

@@ -32,6 +32,7 @@ def tile_attend_s_kernel(tc, q, k, v, out):
         score_banks = ctx.enter_context(tc.psum_pool(name="score_banks", bufs=4))
         turn_banks = ctx.enter_context(tc.psum_pool(name="turn_banks", bufs=2))
         out_banks = ctx.enter_context(tc.psum_pool(name="out_banks", bufs=2))
+        ctx.enter_context(tc.manual_schedule())
 
         k_rows = keep.tile([P, KVH, PACK, D], BF16)
         v_rows = keep.tile([P, KVH, PACK, D], BF16)
@@ -40,22 +41,21 @@ def tile_attend_s_kernel(tc, q, k, v, out):
         def load_keys(rows, src, g):
             nc.sync.dma_start(out=rows[:, g], in_=src[0, g].rearrange("(p t) d -> p t d", t=PACK))
 
-        def load_queries(h):
-            nc.sync.dma_start(out=q_rows[:, h], in_=q[0, h].rearrange("(i r) d -> r i d", r=P))
+        def load_queries(queue, h):
+            queue.dma_start(out=q_rows[:, h], in_=q[0, h].rearrange("(i r) d -> r i d", r=P))
 
+        head_order = [h for g in range(KVH) for h in range(g, H, KVH)]
         load_keys(k_rows, k, 0)
-        load_queries(0)
+        load_queries(nc.scalar, head_order[0])
+        load_queries(nc.sync, head_order[1])
         load_keys(k_rows, k, 1)
-        load_queries(1)
+        load_queries(nc.sync, head_order[2])
         load_keys(v_rows, v, 0)
         load_keys(v_rows, v, 1)
-        load_queries(2)
-        load_queries(3)
+        load_queries(nc.sync, head_order[3])
 
         ident_bf = keep.tile([P, P], BF16)
         make_identity(nc, ident_bf[:])
-        ident_f32 = keep.tile([P, P], F32)
-        make_identity(nc, ident_f32[:])
         causal = keep.tile([P, P], F32)
         nc.gpsimd.memset(causal[:], 0.0)
         nc.gpsimd.affine_select(
@@ -67,11 +67,8 @@ def tile_attend_s_kernel(tc, q, k, v, out):
             pattern=[[-1, P]],
             channel_multiplier=1,
         )
-        causal_bf = keep.tile([P, PAIRS, STEP], BF16)
-        nc.vector.tensor_copy(
-            out=causal_bf[:].rearrange("r u (p e) -> r u p e", e=2),
-            in_=causal[:].rearrange("r (p u e) -> r u p e", u=PAIRS, e=2),
-        )
+        ident_f32 = keep.tile([P, P], F32)
+        make_identity(nc, ident_f32[:])
         warm = keep.tile([P, 1], F32)
         nc.vector.memset(warm[:], 0.0)
         nc.scalar.activation(out=warm[:], in_=warm[:], func=ACT.Exp)
@@ -83,9 +80,9 @@ def tile_attend_s_kernel(tc, q, k, v, out):
         shift = keep.tile([P, H, QT], F32)
         row_sum = keep.tile([P, H, QT], F32)
         inv_sum = keep.tile([P, H, QT], F32)
-        e_grouped = keep.tile([P, H, QT, P, PACK], BF16, align_bytes=64)
-        e_codes = keep.tile([P, H, QT, P], U32, align_bytes=64)
-        e_scales = keep.tile([P, H, QT, P], U8, align_bytes=64)
+        e_grouped = keep.tile([P, H, 2, 2, P, PACK], BF16, align_bytes=64)
+        e_codes = keep.tile([P, H, 2, 2, P], U32, align_bytes=64)
+        e_scales = keep.tile([P, H, 2, 2, P], U8, align_bytes=64)
         v_grouped = keep.tile([P, KVH, D, PACK], BF16, align_bytes=64)
         v_codes = keep.tile([P, KVH, D], U32, align_bytes=64)
         v_scales = keep.tile([P, KVH, D], U8, align_bytes=64)
@@ -93,9 +90,14 @@ def tile_attend_s_kernel(tc, q, k, v, out):
 
         for i in range(QT - 1):
             nc.vector.memset(e_all[:, :, i, :, STEP * (i + 1) :], 0.0)
+        causal_bf = keep.tile([P, PAIRS, STEP], BF16)
+        nc.vector.tensor_copy(
+            out=causal_bf[:].rearrange("r u (p e) -> r u p e", e=2),
+            in_=causal[:].rearrange("r (p u e) -> r u p e", u=PAIRS, e=2),
+        )
 
         def turn_keys(g):
-            kt_ps = turn_banks.tile([P, PACK, P], BF16, tag="turn")
+            kt_ps = out_banks.tile([P, PACK, P], BF16, tag="o")
             for t in range(PACK):
                 nc.tensor.transpose(kt_ps[:, t, :], k_rows[:, g, t, :], ident_bf[:])
             nc.vector.tensor_copy(
@@ -103,11 +105,11 @@ def tile_attend_s_kernel(tc, q, k, v, out):
                 in_=kt_ps[:].rearrange("d (u e) p -> d u p e", e=2),
             )
 
-        def turn_queries(h):
-            qt_ps = turn_banks.tile([P, QT, P], BF16, tag="turn")
+        def turn_queries(h, copy):
+            qt_ps = out_banks.tile([P, QT, P], BF16, tag="o")
             for i in range(QT):
                 nc.tensor.transpose(qt_ps[:, i, :], q_rows[:, h, i, :], ident_bf[:])
-            nc.scalar.copy(out=qT[:, h], in_=qt_ps[:])
+            copy(out=qT[:, h], in_=qt_ps[:])
 
         def quantise_values():
             nc.vector.tensor_copy(out=v_grouped[:], in_=v_rows[:].rearrange("p g t d -> p g d t"))
@@ -117,10 +119,21 @@ def tile_attend_s_kernel(tc, q, k, v, out):
                 in_=v_grouped[:].rearrange("p g d t -> p (g d t)"),
             )
 
-        def softmax_numerators(h, i):
+        units = [(h, j) for h in head_order for j in range(QT // 2)]
+        s_tiles = {}
+        et_tiles = {}
+        o_tiles = {}
+
+        def tiles_of(j):
+            return (j, QT - 1 - j)
+
+        def both(j):
+            return slice(j, QT - j, QT - 1 - 2 * j)
+
+        def scores(h, i):
             cols = STEP * (i + 1)
-            s_ps = score_banks.tile([P, PAIRS, cols], F32, tag="s")
             seen = STEP * i
+            s_ps = score_banks.tile([P, PAIRS, cols], F32, tag="s")
             nc.tensor.matmul(
                 out=s_ps[:, :, seen:], lhsT=ident_bf[:], rhs=causal_bf[:], start=True, stop=False
             )
@@ -139,64 +152,102 @@ def tile_attend_s_kernel(tc, q, k, v, out):
                     start=True,
                     stop=True,
                 )
-            nc.vector.reduce_max(out=row_max[:, h, i : i + 1], in_=s_ps[:], axis=AXIS.XY)
-            nc.scalar.mul(out=shift[:, h, i : i + 1], in_=row_max[:, h, i : i + 1], mul=-SCALE)
+            s_tiles[(h, i)] = s_ps
+
+        def maxima(h, j):
+            for i in tiles_of(j):
+                one = slice(i, i + 1)
+                nc.vector.reduce_max(out=row_max[:, h, one], in_=s_tiles[(h, i)][:], axis=AXIS.XY)
+                nc.gpsimd.tensor_scalar_mul(out=shift[:, h, one], in0=row_max[:, h, one], scalar1=-SCALE)
+
+        def exponentials(h, i):
             nc.scalar.activation(
-                out=e_all[:, h, i, :, :cols],
-                in_=s_ps[:],
+                out=e_all[:, h, i, :, : STEP * (i + 1)],
+                in_=s_tiles[(h, i)][:],
                 func=ACT.Exp,
                 bias=shift[:, h, i : i + 1],
                 scale=SCALE,
                 accum_out=row_sum[:, h, i : i + 1],
             )
 
-        def attend(h, first):
-            two = slice(first, first + 2)
-            e_words = e_all[:, h, two].bitcast(F32)
-            et_ps = turn_banks.tile([P, 2, PAIRS, P], F32, tag="turn")
-            for a in range(2):
-                for u in range(PAIRS):
-                    nc.tensor.transpose(et_ps[:, a, u, :], e_words[:, a, u, :], ident_f32[:])
+        def turn_e(h, j, a):
+            if a == 0:
+                et_tiles[(h, j)] = turn_banks.tile([P, 2, PAIRS, P], F32, tag="turn", name="et_ps")
+            e_words = e_all[:, h, tiles_of(j)[a]].bitcast(F32)
+            for u in range(PAIRS):
+                nc.tensor.transpose(et_tiles[(h, j)][:, a, u, :], e_words[:, u, :], ident_f32[:])
+
+        def regroup(h, j):
             nc.scalar.copy(
-                out=e_grouped[:, h, two].bitcast(F32), in_=et_ps[:].rearrange("p a u r -> p a r u")
+                out=e_grouped[:, h, j].bitcast(F32),
+                in_=et_tiles[(h, j)][:].rearrange("p a u r -> p a r u"),
             )
+
+        def quantise(h, j):
+            nc.vector.reciprocal(out=inv_sum[:, h, both(j)], in_=row_sum[:, h, both(j)])
             nc.vector.quantize_mx(
-                out=e_codes[:, h, two].rearrange("p a r -> p (a r)").bitcast(FP8X4),
-                scales=e_scales[:, h, two].rearrange("p a r -> p (a r)"),
-                in_=e_grouped[:, h, two].rearrange("p a r t -> p (a r t)"),
+                out=e_codes[:, h, j].rearrange("p a r -> p (a r)").bitcast(FP8X4),
+                scales=e_scales[:, h, j].rearrange("p a r -> p (a r)"),
+                in_=e_grouped[:, h, j].rearrange("p a r t -> p (a r t)"),
             )
+
+        def multiply(h, j):
             o_ps = out_banks.tile([P, 2, D], F32, tag="o")
             for a in range(2):
-                i = first + a
                 nc.tensor.matmul_mx(
                     out=o_ps[:, a, :],
-                    lhsT=e_codes[:, h, i, :].bitcast(FP8X4),
-                    lhsT_scale=e_scales[:, h, i, :],
+                    lhsT=e_codes[:, h, j, a, :].bitcast(FP8X4),
+                    lhsT_scale=e_scales[:, h, j, a, :],
                     rhs=v_codes[:, h % KVH, :].bitcast(FP8X4),
                     rhs_scale=v_scales[:, h % KVH, :],
                     start=True,
                     stop=True,
                 )
-            nc.vector.reciprocal(out=inv_sum[:, h, two], in_=row_sum[:, h, two])
+            o_tiles[(h, j)] = o_ps
+
+        def finish(h, j):
             nc.vector.tensor_tensor(
-                out=o_all[:, h, two, :],
-                in0=o_ps[:],
-                in1=inv_sum[:, h, two].unsqueeze(2).to_broadcast([P, 2, D]),
+                out=o_all[:, h, both(j), :],
+                in0=o_tiles[(h, j)][:],
+                in1=inv_sum[:, h, both(j)].unsqueeze(2).to_broadcast([P, 2, D]),
                 op=ALU.mult,
             )
             nc.sync.dma_start(
-                out=out[0, h].rearrange("(i r) d -> r i d", r=P)[:, two, :], in_=o_all[:, h, two, :]
+                out=out[0, h].rearrange("(i r) d -> r i d", r=P)[:, both(j), :],
+                in_=o_all[:, h, both(j), :],
             )
 
+        def is_unit(n):
+            return 0 <= n < len(units)
+
         turn_keys(0)
-        turn_queries(0)
-        turn_keys(1)
-        turn_queries(1)
-        quantise_values()
-        turn_queries(2)
-        turn_queries(3)
-        for h in range(H):
-            for first in range(0, QT, 2):
-                softmax_numerators(h, first)
-                softmax_numerators(h, first + 1)
-                attend(h, first)
+        turn_queries(head_order[0], nc.scalar.copy)
+        turn_queries(head_order[1], nc.scalar.copy)
+        for n in range(-2, len(units) + 3):
+            if is_unit(n - 3):
+                multiply(*units[n - 3])
+            for a in range(2):
+                if is_unit(n):
+                    h, j = units[n]
+                    exponentials(h, tiles_of(j)[a])
+                if is_unit(n + 2):
+                    h, j = units[n + 2]
+                    scores(h, tiles_of(j)[a])
+                if is_unit(n):
+                    h, j = units[n]
+                    turn_e(h, j, a)
+            if is_unit(n + 1):
+                maxima(*units[n + 1])
+            if is_unit(n - 1):
+                regroup(*units[n - 1])
+            if n == 0:
+                turn_keys(1)
+                turn_queries(head_order[2], nc.vector.tensor_copy)
+            if n == 1:
+                quantise_values()
+            if n == 2:
+                turn_queries(head_order[3], nc.vector.tensor_copy)
+            if is_unit(n - 2):
+                quantise(*units[n - 2])
+            if is_unit(n - 3):
+                finish(*units[n - 3])

@@ -96,20 +96,29 @@ def tile_attend_s_kernel(tc, q, k, v, out):
             in_=causal[:].rearrange("r (p u e) -> r u p e", u=PAIRS, e=2),
         )
 
+        kt_tiles = {}
+        qt_tiles = {}
+
         def turn_keys(g):
             kt_ps = out_banks.tile([P, PACK, P], BF16, tag="o")
             for t in range(PACK):
                 nc.tensor.transpose(kt_ps[:, t, :], k_rows[:, g, t, :], ident_bf[:])
+            kt_tiles[g] = kt_ps
+
+        def keep_keys(g):
             nc.vector.tensor_copy(
                 out=kT[:, g].rearrange("d u (p e) -> d u p e", e=2),
-                in_=kt_ps[:].rearrange("d (u e) p -> d u p e", e=2),
+                in_=kt_tiles[g][:].rearrange("d (u e) p -> d u p e", e=2),
             )
 
-        def turn_queries(h, copy):
+        def turn_queries(h):
             qt_ps = out_banks.tile([P, QT, P], BF16, tag="o")
             for i in range(QT):
                 nc.tensor.transpose(qt_ps[:, i, :], q_rows[:, h, i, :], ident_bf[:])
-            copy(out=qT[:, h], in_=qt_ps[:])
+            qt_tiles[h] = qt_ps
+
+        def keep_queries(h, copy):
+            copy(out=qT[:, h], in_=qt_tiles[h][:])
 
         def quantise_values():
             nc.vector.tensor_copy(out=v_grouped[:], in_=v_rows[:].rearrange("p g t d -> p g d t"))
@@ -221,8 +230,10 @@ def tile_attend_s_kernel(tc, q, k, v, out):
             return 0 <= n < len(units)
 
         turn_keys(0)
-        turn_queries(head_order[0], nc.scalar.copy)
-        turn_queries(head_order[1], nc.scalar.copy)
+        keep_keys(0)
+        for h in head_order[:2]:
+            turn_queries(h)
+            keep_queries(h, nc.scalar.copy)
         for n in range(-2, len(units) + 3):
             if is_unit(n - 3):
                 multiply(*units[n - 3])
@@ -240,13 +251,16 @@ def tile_attend_s_kernel(tc, q, k, v, out):
                 maxima(*units[n + 1])
             if is_unit(n - 1):
                 regroup(*units[n - 1])
-            if n == 0:
+            if n == -1:
                 turn_keys(1)
-                turn_queries(head_order[2], nc.vector.tensor_copy)
+                turn_queries(head_order[2])
+            if n == 0:
+                keep_keys(1)
+                keep_queries(head_order[2], nc.vector.tensor_copy)
+                turn_queries(head_order[3])
             if n == 1:
+                keep_queries(head_order[3], nc.vector.tensor_copy)
                 quantise_values()
-            if n == 2:
-                turn_queries(head_order[3], nc.vector.tensor_copy)
             if is_unit(n - 2):
                 quantise(*units[n - 2])
             if is_unit(n - 3):

@@ -105,8 +105,8 @@ def tile_attend_s_kernel(tc, q, k, v, out):
                 nc.tensor.transpose(kt_ps[:, t, :], k_rows[:, g, t, :], ident_bf[:])
             kt_tiles[g] = kt_ps
 
-        def keep_keys(g):
-            nc.vector.tensor_copy(
+        def keep_keys(g, copy):
+            copy(
                 out=kT[:, g].rearrange("d u (p e) -> d u p e", e=2),
                 in_=kt_tiles[g][:].rearrange("d (u e) p -> d u p e", e=2),
             )
@@ -193,7 +193,8 @@ def tile_attend_s_kernel(tc, q, k, v, out):
             )
 
         def quantise(h, j):
-            nc.vector.reciprocal(out=inv_sum[:, h, both(j)], in_=row_sum[:, h, both(j)])
+            if j == QT // 2 - 1:
+                nc.vector.reciprocal(out=inv_sum[:, h, :], in_=row_sum[:, h, :])
             nc.vector.quantize_mx(
                 out=e_codes[:, h, j].rearrange("p a r -> p (a r)").bitcast(FP8X4),
                 scales=e_scales[:, h, j].rearrange("p a r -> p (a r)"),
@@ -230,7 +231,7 @@ def tile_attend_s_kernel(tc, q, k, v, out):
             return 0 <= n < len(units)
 
         turn_keys(0)
-        keep_keys(0)
+        keep_keys(0, nc.vector.tensor_copy)
         for h in head_order[:2]:
             turn_queries(h)
             keep_queries(h, nc.scalar.copy)
@@ -255,11 +256,11 @@ def tile_attend_s_kernel(tc, q, k, v, out):
                 turn_keys(1)
                 turn_queries(head_order[2])
             if n == 0:
-                keep_keys(1)
-                keep_queries(head_order[2], nc.vector.tensor_copy)
+                keep_keys(1, nc.scalar.copy)
+                keep_queries(head_order[2], nc.scalar.copy)
                 turn_queries(head_order[3])
             if n == 1:
-                keep_queries(head_order[3], nc.vector.tensor_copy)
+                keep_queries(head_order[3], nc.scalar.copy)
                 quantise_values()
             if is_unit(n - 2):
                 quantise(*units[n - 2])

@@ -6,6 +6,7 @@ from concourse.masks import make_identity
 F32 = mybir.dt.float32
 BF16 = mybir.dt.bfloat16
 U32 = mybir.dt.uint32
+I32 = mybir.dt.int32
 U8 = mybir.dt.uint8
 FP8X4 = mybir.dt.float8_e4m3fn_x4
 ALU = mybir.AluOpType
@@ -19,14 +20,30 @@ PACK = 4
 PAIRS = PACK // 2
 PAIR_COLS = N // PAIRS
 STEP = P // PAIRS
+QUAD = P // PACK
 SCALE = D ** -0.5
 MASKED = -(2.0 ** 127)
 
 FLOPS = 2 * 2 * H * N * N * D
 
+PLACES = [(0, 3 * QUAD), (2, 0), (1, 0), (1, 2 * QUAD)]
+
+
+def units_of(g):
+    h, other = g, g + KVH
+    return [
+        [(h, 0, 3 * QUAD), (h, 2, 0)],
+        [(h, 3, 0)],
+        [(h, 1, 0), (other, 1, 2 * QUAD)],
+        [(other, 3, 0)],
+        [(other, 0, 3 * QUAD), (other, 2, 0)],
+    ]
+
 
 def tile_attend_s_kernel(tc, q, k, v, out):
     nc = tc.nc
+    units = [unit for g in range(KVH) for unit in units_of(g)]
+    U = len(units)
     with ExitStack() as ctx:
         keep = ctx.enter_context(tc.tile_pool(name="keep", bufs=1))
         score_banks = ctx.enter_context(tc.psum_pool(name="score_banks", bufs=4))
@@ -44,15 +61,14 @@ def tile_attend_s_kernel(tc, q, k, v, out):
         def load_queries(queue, h):
             queue.dma_start(out=q_rows[:, h], in_=q[0, h].rearrange("(i r) d -> r i d", r=P))
 
-        head_order = [h for g in range(KVH) for h in range(g, H, KVH)]
         load_keys(k_rows, k, 0)
-        load_queries(nc.scalar, head_order[0])
-        load_queries(nc.sync, head_order[1])
-        load_keys(k_rows, k, 1)
-        load_queries(nc.sync, head_order[2])
+        load_queries(nc.scalar, 0)
         load_keys(v_rows, v, 0)
+        load_queries(nc.sync, KVH)
+        load_keys(k_rows, k, 1)
+        load_queries(nc.sync, 1)
         load_keys(v_rows, v, 1)
-        load_queries(nc.sync, head_order[3])
+        load_queries(nc.sync, 1 + KVH)
 
         ident_bf = keep.tile([P, P], BF16)
         make_identity(nc, ident_bf[:])
@@ -75,21 +91,24 @@ def tile_attend_s_kernel(tc, q, k, v, out):
 
         kT = keep.tile([P, KVH, PAIRS, PAIR_COLS], BF16)
         qT = keep.tile([P, H, QT, P], BF16)
-        e_all = keep.tile([P, H, QT, PAIRS, PAIR_COLS], BF16)
-        row_max = keep.tile([P, H, QT], F32)
-        shift = keep.tile([P, H, QT], F32)
-        row_sum = keep.tile([P, H, QT], F32)
-        inv_sum = keep.tile([P, H, QT], F32)
-        e_grouped = keep.tile([P, H, 2, 2, P, PACK], BF16, align_bytes=64)
-        e_codes = keep.tile([P, H, 2, 2, P], U32, align_bytes=64)
-        e_scales = keep.tile([P, H, 2, 2, P], U8, align_bytes=64)
+        e_all = keep.tile([P, U, PAIRS, PAIR_COLS], BF16)
+        row_max = keep.tile([P, U, 2], F32)
+        shift = keep.tile([P, U, 2], F32)
+        row_sum = keep.tile([P, U, 2], F32)
+        inv_sum = keep.tile([P, U, 2], F32)
+        e_grouped = keep.tile([P, U, P, PACK], BF16, align_bytes=64)
+        e_codes = keep.tile([P, U, P], U32, align_bytes=64)
+        e_scales = keep.tile([P, U, P], U8, align_bytes=64)
         v_grouped = keep.tile([P, KVH, D, PACK], BF16, align_bytes=64)
         v_codes = keep.tile([P, KVH, D], U32, align_bytes=64)
         v_scales = keep.tile([P, KVH, D], U8, align_bytes=64)
-        o_all = keep.tile([P, H, QT, D], F32)
+        placed_codes = keep.tile([P, KVH, len(PLACES), D], U32, align_bytes=64)
+        placed_scales = keep.tile([P, KVH, len(PLACES), D], U8, align_bytes=64)
+        o_all = keep.tile([P, U, 2, D], F32)
 
-        for i in range(QT - 1):
-            nc.vector.memset(e_all[:, :, i, :, STEP * (i + 1) :], 0.0)
+        nc.vector.memset(placed_codes[:].bitcast(I32), 0)
+        nc.vector.memset(placed_scales[:].bitcast(I32), 0)
+        nc.vector.memset(v_scales[:].bitcast(I32), 0)
         causal_bf = keep.tile([P, PAIRS, STEP], BF16)
         nc.vector.tensor_copy(
             out=causal_bf[:].rearrange("r u (p e) -> r u p e", e=2),
@@ -120,149 +139,169 @@ def tile_attend_s_kernel(tc, q, k, v, out):
         def keep_queries(h, copy):
             copy(out=qT[:, h], in_=qt_tiles[h][:])
 
-        def quantise_values():
-            nc.vector.tensor_copy(out=v_grouped[:], in_=v_rows[:].rearrange("p g t d -> p g d t"))
-            nc.vector.quantize_mx(
-                out=v_codes[:].rearrange("p g d -> p (g d)").bitcast(FP8X4),
-                scales=v_scales[:].rearrange("p g d -> p (g d)"),
-                in_=v_grouped[:].rearrange("p g d t -> p (g d t)"),
-            )
+        def group_values(g):
+            nc.vector.tensor_copy(out=v_grouped[:, g], in_=v_rows[:, g].rearrange("p t d -> p d t"))
 
-        units = [(h, j) for h in head_order for j in range(QT // 2)]
+        def quantise_values(g):
+            nc.vector.quantize_mx(
+                out=v_codes[:, g, :].bitcast(FP8X4),
+                scales=v_scales[:, g, :],
+                in_=v_grouped[:, g].rearrange("p d t -> p (d t)"),
+            )
+            for place, (i, base) in enumerate(PLACES):
+                rows = QUAD * (i + 1)
+                nc.sync.dma_start(
+                    out=placed_codes[base : base + rows, g, place, :].bitcast(I32),
+                    in_=v_codes[:rows, g, :].bitcast(I32),
+                )
+                nc.sync.dma_start(
+                    out=placed_scales[base : base + rows, g, place, :].bitcast(I32),
+                    in_=v_scales[:rows, g, :].bitcast(I32),
+                )
+
         s_tiles = {}
         et_tiles = {}
         o_tiles = {}
 
-        def tiles_of(j):
-            return (j, QT - 1 - j)
+        def columns(i, base):
+            return slice(2 * base, 2 * base + STEP * (i + 1))
 
-        def both(j):
-            return slice(j, QT - j, QT - 1 - 2 * j)
+        def scores(n):
+            s_ps = score_banks.tile([P, PAIRS, PAIR_COLS], F32, tag="s")
+            for h, i, base in units[n]:
+                first = 2 * base
+                seen = STEP * i
+                diagonal = s_ps[:, :, first + seen : first + seen + STEP]
+                nc.tensor.matmul(out=diagonal, lhsT=ident_bf[:], rhs=causal_bf[:], start=True, stop=False)
+                nc.tensor.matmul(
+                    out=diagonal,
+                    lhsT=qT[:, h, i, :],
+                    rhs=kT[:, h % KVH, :, seen : seen + STEP],
+                    start=False,
+                    stop=True,
+                )
+                if seen > 0:
+                    nc.tensor.matmul(
+                        out=s_ps[:, :, first : first + seen],
+                        lhsT=qT[:, h, i, :],
+                        rhs=kT[:, h % KVH, :, :seen],
+                        start=True,
+                        stop=True,
+                    )
+            s_tiles[n] = s_ps
 
-        def scores(h, i):
-            cols = STEP * (i + 1)
-            seen = STEP * i
-            s_ps = score_banks.tile([P, PAIRS, cols], F32, tag="s")
-            nc.tensor.matmul(
-                out=s_ps[:, :, seen:], lhsT=ident_bf[:], rhs=causal_bf[:], start=True, stop=False
+        def maxima(n):
+            for m, (h, i, base) in enumerate(units[n]):
+                one = slice(m, m + 1)
+                nc.vector.reduce_max(
+                    out=row_max[:, n, one], in_=s_tiles[n][:, :, columns(i, base)], axis=AXIS.XY
+                )
+                nc.gpsimd.tensor_scalar_mul(out=shift[:, n, one], in0=row_max[:, n, one], scalar1=-SCALE)
+
+        def exponentials(n):
+            for m, (h, i, base) in enumerate(units[n]):
+                nc.scalar.activation(
+                    out=e_all[:, n, :, columns(i, base)],
+                    in_=s_tiles[n][:, :, columns(i, base)],
+                    func=ACT.Exp,
+                    bias=shift[:, n, m : m + 1],
+                    scale=SCALE,
+                    accum_out=row_sum[:, n, m : m + 1],
+                )
+
+        def turn_e(n):
+            et_ps = turn_banks.tile([P, PAIRS, P], F32, tag="turn")
+            e_words = e_all[:, n].bitcast(F32)
+            for u in range(PAIRS):
+                nc.tensor.transpose(et_ps[:, u, :], e_words[:, u, :], ident_f32[:])
+            et_tiles[n] = et_ps
+
+        def regroup(n):
+            nc.scalar.copy(
+                out=e_grouped[:, n].bitcast(F32), in_=et_tiles[n][:].rearrange("w u r -> w r u")
             )
-            nc.tensor.matmul(
-                out=s_ps[:, :, seen:],
-                lhsT=qT[:, h, i, :],
-                rhs=kT[:, h % KVH, :, seen:cols],
-                start=False,
+
+        def quantise(n):
+            members = len(units[n])
+            nc.vector.reciprocal(out=inv_sum[:, n, :members], in_=row_sum[:, n, :members])
+            nc.vector.quantize_mx(
+                out=e_codes[:, n, :].bitcast(FP8X4),
+                scales=e_scales[:, n, :],
+                in_=e_grouped[:, n].rearrange("w r t -> w (r t)"),
+            )
+
+        def multiply(n):
+            o_ps = out_banks.tile([P, 2, D], F32, tag="o")
+            h, i, base = units[n][0]
+            g = h % KVH
+            if len(units[n]) == 1:
+                product = o_ps[:, 0, :]
+                values = v_codes[:, g, :]
+                value_scales = v_scales[:, g, :]
+            else:
+                place = PLACES.index((i, base))
+                product = o_ps[:].rearrange("r m d -> r (m d)")
+                values = placed_codes[:, g, place : place + 2, :].rearrange("p m d -> p (m d)")
+                value_scales = placed_scales[:, g, place : place + 2, :].rearrange("p m d -> p (m d)")
+            nc.tensor.matmul_mx(
+                out=product,
+                lhsT=e_codes[:, n, :].bitcast(FP8X4),
+                lhsT_scale=e_scales[:, n, :],
+                rhs=values.bitcast(FP8X4),
+                rhs_scale=value_scales,
+                start=True,
                 stop=True,
             )
-            if seen > 0:
-                nc.tensor.matmul(
-                    out=s_ps[:, :, :seen],
-                    lhsT=qT[:, h, i, :],
-                    rhs=kT[:, h % KVH, :, :seen],
-                    start=True,
-                    stop=True,
-                )
-            s_tiles[(h, i)] = s_ps
+            o_tiles[n] = o_ps
 
-        def maxima(h, j):
-            for i in tiles_of(j):
-                one = slice(i, i + 1)
-                nc.vector.reduce_max(out=row_max[:, h, one], in_=s_tiles[(h, i)][:], axis=AXIS.XY)
-                nc.gpsimd.tensor_scalar_mul(out=shift[:, h, one], in0=row_max[:, h, one], scalar1=-SCALE)
-
-        def exponentials(h, i):
-            nc.scalar.activation(
-                out=e_all[:, h, i, :, : STEP * (i + 1)],
-                in_=s_tiles[(h, i)][:],
-                func=ACT.Exp,
-                bias=shift[:, h, i : i + 1],
-                scale=SCALE,
-                accum_out=row_sum[:, h, i : i + 1],
-            )
-
-        def turn_e(h, j, a):
-            if a == 0:
-                et_tiles[(h, j)] = turn_banks.tile([P, 2, PAIRS, P], F32, tag="turn", name="et_ps")
-            e_words = e_all[:, h, tiles_of(j)[a]].bitcast(F32)
-            for u in range(PAIRS):
-                nc.tensor.transpose(et_tiles[(h, j)][:, a, u, :], e_words[:, u, :], ident_f32[:])
-
-        def regroup(h, j):
-            nc.scalar.copy(
-                out=e_grouped[:, h, j].bitcast(F32),
-                in_=et_tiles[(h, j)][:].rearrange("p a u r -> p a r u"),
-            )
-
-        def quantise(h, j):
-            if j == QT // 2 - 1:
-                nc.vector.reciprocal(out=inv_sum[:, h, :], in_=row_sum[:, h, :])
-            nc.vector.quantize_mx(
-                out=e_codes[:, h, j].rearrange("p a r -> p (a r)").bitcast(FP8X4),
-                scales=e_scales[:, h, j].rearrange("p a r -> p (a r)"),
-                in_=e_grouped[:, h, j].rearrange("p a r t -> p (a r t)"),
-            )
-
-        def multiply(h, j):
-            o_ps = out_banks.tile([P, 2, D], F32, tag="o")
-            for a in range(2):
-                nc.tensor.matmul_mx(
-                    out=o_ps[:, a, :],
-                    lhsT=e_codes[:, h, j, a, :].bitcast(FP8X4),
-                    lhsT_scale=e_scales[:, h, j, a, :],
-                    rhs=v_codes[:, h % KVH, :].bitcast(FP8X4),
-                    rhs_scale=v_scales[:, h % KVH, :],
-                    start=True,
-                    stop=True,
-                )
-            o_tiles[(h, j)] = o_ps
-
-        def finish(h, j):
+        def finish(n):
+            members = len(units[n])
             nc.vector.tensor_tensor(
-                out=o_all[:, h, both(j), :],
-                in0=o_tiles[(h, j)][:],
-                in1=inv_sum[:, h, both(j)].unsqueeze(2).to_broadcast([P, 2, D]),
+                out=o_all[:, n, :members, :],
+                in0=o_tiles[n][:, :members, :],
+                in1=inv_sum[:, n, :members].unsqueeze(2).to_broadcast([P, members, D]),
                 op=ALU.mult,
             )
-            nc.sync.dma_start(
-                out=out[0, h].rearrange("(i r) d -> r i d", r=P)[:, both(j), :],
-                in_=o_all[:, h, both(j), :],
-            )
+            for m, (h, i, base) in enumerate(units[n]):
+                nc.sync.dma_start(out=out[0, h, P * i : P * (i + 1), :], in_=o_all[:, n, m, :])
 
         def is_unit(n):
-            return 0 <= n < len(units)
+            return 0 <= n < U
 
         turn_keys(0)
         keep_keys(0, nc.vector.tensor_copy)
-        for h in head_order[:2]:
-            turn_queries(h)
-            keep_queries(h, nc.scalar.copy)
-        for n in range(-2, len(units) + 3):
+        turn_queries(0)
+        keep_queries(0, nc.scalar.copy)
+        group_values(0)
+        turn_queries(KVH)
+        keep_queries(KVH, nc.scalar.copy)
+        quantise_values(0)
+        for n in range(-2, U + 3):
             if is_unit(n - 3):
-                multiply(*units[n - 3])
-            for a in range(2):
-                if is_unit(n):
-                    h, j = units[n]
-                    exponentials(h, tiles_of(j)[a])
-                if is_unit(n + 2):
-                    h, j = units[n + 2]
-                    scores(h, tiles_of(j)[a])
-                if is_unit(n):
-                    h, j = units[n]
-                    turn_e(h, j, a)
+                multiply(n - 3)
+            if is_unit(n + 2):
+                scores(n + 2)
+            if is_unit(n):
+                exponentials(n)
+                turn_e(n)
             if is_unit(n + 1):
-                maxima(*units[n + 1])
+                maxima(n + 1)
             if is_unit(n - 1):
-                regroup(*units[n - 1])
+                regroup(n - 1)
             if n == -1:
                 turn_keys(1)
-                turn_queries(head_order[2])
             if n == 0:
                 keep_keys(1, nc.scalar.copy)
-                keep_queries(head_order[2], nc.scalar.copy)
-                turn_queries(head_order[3])
+                turn_queries(1)
             if n == 1:
-                keep_queries(head_order[3], nc.scalar.copy)
-                quantise_values()
+                keep_queries(1, nc.scalar.copy)
+                turn_queries(1 + KVH)
+            if n == 2:
+                keep_queries(1 + KVH, nc.scalar.copy)
+                group_values(1)
+            if n == 3:
+                quantise_values(1)
             if is_unit(n - 2):
-                quantise(*units[n - 2])
+                quantise(n - 2)
             if is_unit(n - 3):
-                finish(*units[n - 3])
+                finish(n - 3)

@@ -32,11 +32,11 @@ PLACES = [(0, 3 * QUAD), (2, 0), (1, 0), (1, 2 * QUAD)]
 def units_of(g):
     h, other = g, g + KVH
     return [
-        [(h, 0, 3 * QUAD), (h, 2, 0)],
         [(h, 3, 0)],
+        [(h, 0, 3 * QUAD), (h, 2, 0)],
         [(h, 1, 0), (other, 1, 2 * QUAD)],
-        [(other, 3, 0)],
         [(other, 0, 3 * QUAD), (other, 2, 0)],
+        [(other, 3, 0)],
     ]
 
 
@@ -64,10 +64,10 @@ def tile_attend_s_kernel(tc, q, k, v, out):
         load_keys(k_rows, k, 0)
         load_queries(nc.scalar, 0)
         load_keys(v_rows, v, 0)
+        load_keys(v_rows, v, 1)
         load_queries(nc.sync, KVH)
         load_keys(k_rows, k, 1)
         load_queries(nc.sync, 1)
-        load_keys(v_rows, v, 1)
         load_queries(nc.sync, 1 + KVH)
 
         ident_bf = keep.tile([P, P], BF16)
@@ -109,54 +109,52 @@ def tile_attend_s_kernel(tc, q, k, v, out):
         nc.vector.memset(placed_codes[:].bitcast(I32), 0)
         nc.vector.memset(placed_scales[:].bitcast(I32), 0)
         nc.vector.memset(v_scales[:].bitcast(I32), 0)
+        nc.vector.memset(row_sum[:], 1.0)
         causal_bf = keep.tile([P, PAIRS, STEP], BF16)
         nc.vector.tensor_copy(
             out=causal_bf[:].rearrange("r u (p e) -> r u p e", e=2),
             in_=causal[:].rearrange("r (p u e) -> r u p e", u=PAIRS, e=2),
         )
 
-        kt_tiles = {}
-        qt_tiles = {}
+        def turn_keys(g, u, count):
+            kt_ps = out_banks.tile([P, 2 * count, P], BF16, tag="o")
+            for t in range(2 * count):
+                nc.tensor.transpose(kt_ps[:, t, :], k_rows[:, g, 2 * u + t, :], ident_bf[:])
+            return kt_ps
 
-        def turn_keys(g):
-            kt_ps = out_banks.tile([P, PACK, P], BF16, tag="o")
-            for t in range(PACK):
-                nc.tensor.transpose(kt_ps[:, t, :], k_rows[:, g, t, :], ident_bf[:])
-            kt_tiles[g] = kt_ps
-
-        def keep_keys(g, copy):
+        def keep_keys(kt_ps, g, u, count, copy):
             copy(
-                out=kT[:, g].rearrange("d u (p e) -> d u p e", e=2),
-                in_=kt_tiles[g][:].rearrange("d (u e) p -> d u p e", e=2),
+                out=kT[:, g, u : u + count].rearrange("d u (p e) -> d u p e", e=2),
+                in_=kt_ps[:].rearrange("d (u e) p -> d u p e", e=2),
             )
 
-        def turn_queries(h):
-            qt_ps = out_banks.tile([P, QT, P], BF16, tag="o")
-            for i in range(QT):
-                nc.tensor.transpose(qt_ps[:, i, :], q_rows[:, h, i, :], ident_bf[:])
-            qt_tiles[h] = qt_ps
+        def turn_queries(banks, tag, h, i, count):
+            qt_ps = banks.tile([P, count, P], BF16, tag=tag)
+            for c in range(count):
+                nc.tensor.transpose(qt_ps[:, c, :], q_rows[:, h, i + c, :], ident_bf[:])
+            return qt_ps
 
-        def keep_queries(h, copy):
-            copy(out=qT[:, h], in_=qt_tiles[h][:])
+        def keep_queries(qt_ps, h, i, count, copy):
+            copy(out=qT[:, h, i : i + count], in_=qt_ps[:])
 
-        def group_values(g):
-            nc.vector.tensor_copy(out=v_grouped[:, g], in_=v_rows[:, g].rearrange("p t d -> p d t"))
+        def group_values():
+            nc.vector.tensor_copy(out=v_grouped[:], in_=v_rows[:].rearrange("p g t d -> p g d t"))
 
-        def quantise_values(g):
+        def quantise_values():
             nc.vector.quantize_mx(
-                out=v_codes[:, g, :].bitcast(FP8X4),
-                scales=v_scales[:, g, :],
-                in_=v_grouped[:, g].rearrange("p d t -> p (d t)"),
+                out=v_codes[:].rearrange("p g d -> p (g d)").bitcast(FP8X4),
+                scales=v_scales[:].rearrange("p g d -> p (g d)"),
+                in_=v_grouped[:].rearrange("p g d t -> p (g d t)"),
             )
             for place, (i, base) in enumerate(PLACES):
                 rows = QUAD * (i + 1)
                 nc.sync.dma_start(
-                    out=placed_codes[base : base + rows, g, place, :].bitcast(I32),
-                    in_=v_codes[:rows, g, :].bitcast(I32),
+                    out=placed_codes[base : base + rows, :, place, :].bitcast(I32),
+                    in_=v_codes[:rows].bitcast(I32),
                 )
                 nc.sync.dma_start(
-                    out=placed_scales[base : base + rows, g, place, :].bitcast(I32),
-                    in_=v_scales[:rows, g, :].bitcast(I32),
+                    out=placed_scales[base : base + rows, :, place, :].bitcast(I32),
+                    in_=v_scales[:rows].bitcast(I32),
                 )
 
         s_tiles = {}
@@ -190,13 +188,13 @@ def tile_attend_s_kernel(tc, q, k, v, out):
                     )
             s_tiles[n] = s_ps
 
-        def maxima(n):
+        def maxima(n, engine):
+            members = len(units[n])
             for m, (h, i, base) in enumerate(units[n]):
-                one = slice(m, m + 1)
                 nc.vector.reduce_max(
-                    out=row_max[:, n, one], in_=s_tiles[n][:, :, columns(i, base)], axis=AXIS.XY
+                    out=row_max[:, n, m : m + 1], in_=s_tiles[n][:, :, columns(i, base)], axis=AXIS.XY
                 )
-                nc.gpsimd.tensor_scalar_mul(out=shift[:, n, one], in0=row_max[:, n, one], scalar1=-SCALE)
+            engine.tensor_scalar_mul(out=shift[:, n, :members], in0=row_max[:, n, :members], scalar1=-SCALE)
 
         def exponentials(n):
             for m, (h, i, base) in enumerate(units[n]):
@@ -221,9 +219,10 @@ def tile_attend_s_kernel(tc, q, k, v, out):
                 out=e_grouped[:, n].bitcast(F32), in_=et_tiles[n][:].rearrange("w u r -> w r u")
             )
 
+        def invert(first, end):
+            nc.vector.reciprocal(out=inv_sum[:, first:end, :], in_=row_sum[:, first:end, :])
+
         def quantise(n):
-            members = len(units[n])
-            nc.vector.reciprocal(out=inv_sum[:, n, :members], in_=row_sum[:, n, :members])
             nc.vector.quantize_mx(
                 out=e_codes[:, n, :].bitcast(FP8X4),
                 scales=e_scales[:, n, :],
@@ -268,39 +267,45 @@ def tile_attend_s_kernel(tc, q, k, v, out):
         def is_unit(n):
             return 0 <= n < U
 
-        turn_keys(0)
-        keep_keys(0, nc.vector.tensor_copy)
-        turn_queries(0)
-        keep_queries(0, nc.scalar.copy)
-        group_values(0)
-        turn_queries(KVH)
-        keep_queries(KVH, nc.scalar.copy)
-        quantise_values(0)
-        for n in range(-2, U + 3):
+        first_k = turn_keys(0, 0, 1)
+        keep_keys(first_k, 0, 0, 1, nc.vector.tensor_copy)
+        second_k = turn_keys(0, 1, 1)
+        keep_keys(second_k, 0, 1, 1, nc.scalar.copy)
+        first_q = turn_queries(turn_banks, "turn", 0, QT - 1, 1)
+        keep_queries(first_q, 0, QT - 1, 1, nc.vector.tensor_copy)
+        other_q = turn_queries(turn_banks, "turn", 0, 0, QT - 1)
+        keep_queries(other_q, 0, 0, QT - 1, nc.scalar.copy)
+        group_values()
+        turned = {}
+        for n in range(-3, U + 3):
             if is_unit(n - 3):
                 multiply(n - 3)
-            if is_unit(n + 2):
-                scores(n + 2)
+            if is_unit(n + 3):
+                scores(n + 3)
             if is_unit(n):
                 exponentials(n)
                 turn_e(n)
-            if is_unit(n + 1):
-                maxima(n + 1)
+            if is_unit(n + 2):
+                maxima(n + 2, nc.vector if n + 2 == 0 else nc.gpsimd)
             if is_unit(n - 1):
                 regroup(n - 1)
+            if n == -3:
+                turned["q"] = turn_queries(out_banks, "o", KVH, 0, QT)
+                keep_queries(turned["q"], KVH, 0, QT, nc.scalar.copy)
+            if n == -2:
+                quantise_values()
+                turned["k"] = turn_keys(1, 0, PAIRS)
             if n == -1:
-                turn_keys(1)
+                turned["q"] = turn_queries(out_banks, "o", 1, 0, QT)
             if n == 0:
-                keep_keys(1, nc.scalar.copy)
-                turn_queries(1)
+                keep_keys(turned["k"], 1, 0, PAIRS, nc.scalar.copy)
             if n == 1:
-                keep_queries(1, nc.scalar.copy)
-                turn_queries(1 + KVH)
+                keep_queries(turned["q"], 1, 0, QT, nc.scalar.copy)
+                turned["q"] = turn_queries(out_banks, "o", 1 + KVH, 0, QT)
             if n == 2:
-                keep_queries(1 + KVH, nc.scalar.copy)
-                group_values(1)
-            if n == 3:
-                quantise_values(1)
+                keep_queries(turned["q"], 1 + KVH, 0, QT, nc.scalar.copy)
+            if is_unit(n - 3) and (n - 3) % 3 == 0:
+                invert(n - 3, min(n, U))
             if is_unit(n - 2):
                 quantise(n - 2)
             if is_unit(n - 3):

@@ -72,6 +72,11 @@ def tile_attend_s_kernel(tc, q, k, v, out):
 
         ident_bf = keep.tile([P, P], BF16)
         make_identity(nc, ident_bf[:])
+        idle_rhs = keep.tile([P, N], BF16)
+        nc.vector.memset(idle_rhs[:].bitcast(F32), 0.0)
+        idle_ps = score_banks.tile([P, N], F32, tag="s")
+        for repeat in range(3):
+            nc.tensor.matmul(out=idle_ps[:], lhsT=ident_bf[:], rhs=idle_rhs[:], start=True, stop=True)
         causal = keep.tile([P, P], F32)
         nc.gpsimd.memset(causal[:], 0.0)
         nc.gpsimd.affine_select(
@@ -304,8 +309,10 @@ def tile_attend_s_kernel(tc, q, k, v, out):
                 turned["q"] = turn_queries(out_banks, "o", 1 + KVH, 0, QT)
             if n == 2:
                 keep_queries(turned["q"], 1 + KVH, 0, QT, nc.scalar.copy)
-            if is_unit(n - 3) and (n - 3) % 3 == 0:
-                invert(n - 3, min(n, U))
+            if n == 3:
+                invert(0, 1)
+            if is_unit(n - 3) and (n - 3) % 3 == 1:
+                invert(n - 3, n)
             if is_unit(n - 2):
                 quantise(n - 2)
             if is_unit(n - 3):

@@ -63,9 +63,9 @@ def tile_attend_s_kernel(tc, q, k, v, out):
 
         load_keys(k_rows, k, 0)
         load_queries(nc.scalar, 0)
+        load_queries(nc.sync, KVH)
         load_keys(v_rows, v, 0)
         load_keys(v_rows, v, 1)
-        load_queries(nc.sync, KVH)
         load_keys(k_rows, k, 1)
         load_queries(nc.sync, 1)
         load_queries(nc.sync, 1 + KVH)
@@ -142,8 +142,15 @@ def tile_attend_s_kernel(tc, q, k, v, out):
         def keep_queries(qt_ps, h, i, count, copy):
             copy(out=qT[:, h, i : i + count], in_=qt_ps[:])
 
-        def group_values():
-            nc.vector.tensor_copy(out=v_grouped[:], in_=v_rows[:].rearrange("p g t d -> p g d t"))
+        def group_values(g):
+            nc.gpsimd.tensor_scalar(
+                out=v_grouped[:, g],
+                in0=v_rows[:, g].rearrange("p t d -> p d t"),
+                scalar1=1.0,
+                scalar2=0.0,
+                op0=ALU.mult,
+                op1=ALU.add,
+            )
 
         def quantise_values():
             nc.vector.quantize_mx(
@@ -153,14 +160,18 @@ def tile_attend_s_kernel(tc, q, k, v, out):
             )
             for place, (i, base) in enumerate(PLACES):
                 rows = QUAD * (i + 1)
-                nc.sync.dma_start(
-                    out=placed_codes[base : base + rows, :, place, :].bitcast(I32),
-                    in_=v_codes[:rows].bitcast(I32),
-                )
-                nc.sync.dma_start(
-                    out=placed_scales[base : base + rows, :, place, :].bitcast(I32),
-                    in_=v_scales[:rows].bitcast(I32),
-                )
+                start = 0
+                for size in (2 * QUAD, QUAD):
+                    if rows - start >= size:
+                        nc.sync.dma_start(
+                            out=placed_codes[base + start : base + start + size, :, place, :].bitcast(I32),
+                            in_=v_codes[start : start + size].bitcast(I32),
+                        )
+                        nc.sync.dma_start(
+                            out=placed_scales[base + start : base + start + size, :, place, :].bitcast(I32),
+                            in_=v_scales[start : start + size].bitcast(I32),
+                        )
+                        start += size
 
         s_tiles = {}
         et_tiles = {}
@@ -193,13 +204,20 @@ def tile_attend_s_kernel(tc, q, k, v, out):
                     )
             s_tiles[n] = s_ps
 
-        def maxima(n, engine):
-            members = len(units[n])
+        def maxima(n):
             for m, (h, i, base) in enumerate(units[n]):
                 nc.vector.reduce_max(
                     out=row_max[:, n, m : m + 1], in_=s_tiles[n][:, :, columns(i, base)], axis=AXIS.XY
                 )
-            engine.tensor_scalar_mul(out=shift[:, n, :members], in0=row_max[:, n, :members], scalar1=-SCALE)
+
+        def shifts(n):
+            members = len(units[n])
+            if n == 0:
+                nc.scalar.mul(out=shift[:, n, :members], in_=row_max[:, n, :members], mul=-SCALE)
+            else:
+                nc.gpsimd.tensor_scalar_mul(
+                    out=shift[:, n, :members], in0=row_max[:, n, :members], scalar1=-SCALE
+                )
 
         def exponentials(n):
             for m, (h, i, base) in enumerate(units[n]):
@@ -280,8 +298,11 @@ def tile_attend_s_kernel(tc, q, k, v, out):
         keep_queries(first_q, 0, QT - 1, 1, nc.vector.tensor_copy)
         other_q = turn_queries(turn_banks, "turn", 0, 0, QT - 1)
         keep_queries(other_q, 0, 0, QT - 1, nc.scalar.copy)
-        group_values()
         turned = {}
+        turned["q"] = turn_queries(out_banks, "o", KVH, 0, QT)
+        keep_queries(turned["q"], KVH, 0, QT, nc.scalar.copy)
+        for g in range(KVH):
+            group_values(g)
         for n in range(-3, U + 3):
             if is_unit(n - 3):
                 multiply(n - 3)
@@ -291,19 +312,16 @@ def tile_attend_s_kernel(tc, q, k, v, out):
                 exponentials(n)
                 turn_e(n)
             if is_unit(n + 2):
-                maxima(n + 2, nc.vector if n + 2 == 0 else nc.gpsimd)
+                maxima(n + 2)
+                shifts(n + 2)
             if is_unit(n - 1):
                 regroup(n - 1)
-            if n == -3:
-                turned["q"] = turn_queries(out_banks, "o", KVH, 0, QT)
-                keep_queries(turned["q"], KVH, 0, QT, nc.scalar.copy)
-            if n == -2:
+            if n == -1:
                 quantise_values()
                 turned["k"] = turn_keys(1, 0, PAIRS)
-            if n == -1:
-                turned["q"] = turn_queries(out_banks, "o", 1, 0, QT)
             if n == 0:
                 keep_keys(turned["k"], 1, 0, PAIRS, nc.scalar.copy)
+                turned["q"] = turn_queries(out_banks, "o", 1, 0, QT)
             if n == 1:
                 keep_queries(turned["q"], 1, 0, QT, nc.scalar.copy)
                 turned["q"] = turn_queries(out_banks, "o", 1 + KVH, 0, QT)

@@ -70,13 +70,13 @@ def tile_attend_s_kernel(tc, q, k, v, out):
         load_queries(nc.sync, 1)
         load_queries(nc.sync, 1 + KVH)
 
-        ident_bf = keep.tile([P, P], BF16)
-        make_identity(nc, ident_bf[:])
-        idle_rhs = keep.tile([P, N], BF16)
-        nc.vector.memset(idle_rhs[:].bitcast(F32), 0.0)
+        zeros = keep.tile([P, N], BF16)
+        nc.vector.memset(zeros[:].bitcast(F32), 0.0)
         idle_ps = score_banks.tile([P, N], F32, tag="s")
         for repeat in range(3):
-            nc.tensor.matmul(out=idle_ps[:], lhsT=ident_bf[:], rhs=idle_rhs[:], start=True, stop=True)
+            nc.tensor.matmul(out=idle_ps[:], lhsT=zeros[:, :P], rhs=zeros[:], start=True, stop=True)
+        ident_bf = keep.tile([P, P], BF16)
+        make_identity(nc, ident_bf[:])
         causal = keep.tile([P, P], F32)
         nc.gpsimd.memset(causal[:], 0.0)
         nc.gpsimd.affine_select(
@@ -152,11 +152,11 @@ def tile_attend_s_kernel(tc, q, k, v, out):
                 op1=ALU.add,
             )
 
-        def quantise_values():
+        def quantise_values(g):
             nc.vector.quantize_mx(
-                out=v_codes[:].rearrange("p g d -> p (g d)").bitcast(FP8X4),
-                scales=v_scales[:].rearrange("p g d -> p (g d)"),
-                in_=v_grouped[:].rearrange("p g d t -> p (g d t)"),
+                out=v_codes[:, g, :].bitcast(FP8X4),
+                scales=v_scales[:, g, :],
+                in_=v_grouped[:, g].rearrange("p d t -> p (d t)"),
             )
             for place, (i, base) in enumerate(PLACES):
                 rows = QUAD * (i + 1)
@@ -164,12 +164,12 @@ def tile_attend_s_kernel(tc, q, k, v, out):
                 for size in (2 * QUAD, QUAD):
                     if rows - start >= size:
                         nc.sync.dma_start(
-                            out=placed_codes[base + start : base + start + size, :, place, :].bitcast(I32),
-                            in_=v_codes[start : start + size].bitcast(I32),
+                            out=placed_codes[base + start : base + start + size, g, place, :].bitcast(I32),
+                            in_=v_codes[start : start + size, g, :].bitcast(I32),
                         )
                         nc.sync.dma_start(
-                            out=placed_scales[base + start : base + start + size, :, place, :].bitcast(I32),
-                            in_=v_scales[start : start + size].bitcast(I32),
+                            out=placed_scales[base + start : base + start + size, g, place, :].bitcast(I32),
+                            in_=v_scales[start : start + size, g, :].bitcast(I32),
                         )
                         start += size
 
@@ -308,6 +308,10 @@ def tile_attend_s_kernel(tc, q, k, v, out):
                 multiply(n - 3)
             if is_unit(n + 3):
                 scores(n + 3)
+            if n == 0:
+                turned["q"] = turn_queries(out_banks, "o", 1, 0, QT)
+            if n == 1:
+                turned["q"] = turn_queries(out_banks, "o", 1 + KVH, 0, QT)
             if is_unit(n):
                 exponentials(n)
                 turn_e(n)
@@ -316,16 +320,15 @@ def tile_attend_s_kernel(tc, q, k, v, out):
                 shifts(n + 2)
             if is_unit(n - 1):
                 regroup(n - 1)
+            if n == -2:
+                quantise_values(0)
             if n == -1:
-                quantise_values()
                 turned["k"] = turn_keys(1, 0, PAIRS)
             if n == 0:
+                quantise_values(1)
                 keep_keys(turned["k"], 1, 0, PAIRS, nc.scalar.copy)
-                turned["q"] = turn_queries(out_banks, "o", 1, 0, QT)
-            if n == 1:
                 keep_queries(turned["q"], 1, 0, QT, nc.scalar.copy)
-                turned["q"] = turn_queries(out_banks, "o", 1 + KVH, 0, QT)
-            if n == 2:
+            if n == 1:
                 keep_queries(turned["q"], 1 + KVH, 0, QT, nc.scalar.copy)
             if n == 3:
                 invert(0, 1)

@@ -327,9 +327,9 @@ def tile_attend_s_kernel(tc, q, k, v, out):
             if n == 0:
                 quantise_values(1)
                 keep_keys(turned["k"], 1, 0, PAIRS, nc.scalar.copy)
-                keep_queries(turned["q"], 1, 0, QT, nc.scalar.copy)
+                keep_queries(turned["q"], 1, 0, QT, nc.vector.tensor_copy)
             if n == 1:
-                keep_queries(turned["q"], 1 + KVH, 0, QT, nc.scalar.copy)
+                keep_queries(turned["q"], 1 + KVH, 0, QT, nc.vector.tensor_copy)
             if n == 3:
                 invert(0, 1)
             if is_unit(n - 3) and (n - 3) % 3 == 1:

@@ -15,35 +15,63 @@ AXIS = mybir.AxisListType
 
 P = 128
 H, KVH, N, D = 4, 2, 512, 128
+GROUP = H // KVH
 QT = N // P
+BQ = P // GROUP
+BANDS = N // BQ
 PACK = 4
 PAIRS = PACK // 2
 PAIR_COLS = N // PAIRS
-STEP = P // PAIRS
-QUAD = P // PACK
+BW = BQ // PACK
+STEP = 2 * BW
 SCALE = D ** -0.5
 MASKED = -(2.0 ** 127)
+ROW = D + D // PACK
 
 FLOPS = 2 * 2 * H * N * N * D
 
-PLACES = [(0, 3 * QUAD), (2, 0), (1, 0), (1, 2 * QUAD)]
+HIGH = {6: 0, 5: 1, 4: 2, 3: 3}
+LOW = {0: 4, 1: 5, 2: 6}
+COPIES = len(HIGH) + len(LOW)
 
 
-def units_of(g):
-    h, other = g, g + KVH
-    return [
-        [(h, 3, 0)],
-        [(h, 0, 3 * QUAD), (h, 2, 0)],
-        [(h, 1, 0), (other, 1, 2 * QUAD)],
-        [(other, 0, 3 * QUAD), (other, 2, 0)],
-        [(other, 3, 0)],
-    ]
+def member(g, j, seen, own):
+    return (g, j, seen, own)
+
+
+def high(g, j):
+    return member(g, j, 0, BW * j)
+
+
+LOW_PLACES = {0: (P - BW, P - BW), 1: (P - 2 * BW, P - BW), 2: (P - 2 * BW, P - 3 * BW)}
+
+
+def low(g, j):
+    return member(g, j, LOW_PLACES[j][0], LOW_PLACES[j][1])
+
+
+UNITS = [
+    [high(0, 7)],
+    [low(0, 0), high(0, 6)],
+    [low(0, 1), high(0, 5)],
+    [low(0, 2), high(0, 4)],
+    [high(0, 3), member(1, 3, P // 2, P // 2 + 3 * BW)],
+    [low(1, 2), high(1, 4)],
+    [low(1, 1), high(1, 5)],
+    [low(1, 0), high(1, 6)],
+    [high(1, 7)],
+]
+
+
+def columns(band):
+    g, j, seen, own = band
+    first = 2 * (own if j == 0 else min(seen, own))
+    return slice(first, first + STEP * (j + 1))
 
 
 def tile_attend_s_kernel(tc, q, k, v, out):
     nc = tc.nc
-    units = [unit for g in range(KVH) for unit in units_of(g)]
-    U = len(units)
+    U = len(UNITS)
     with ExitStack() as ctx:
         keep = ctx.enter_context(tc.tile_pool(name="keep", bufs=1))
         score_banks = ctx.enter_context(tc.psum_pool(name="score_banks", bufs=4))
@@ -53,22 +81,33 @@ def tile_attend_s_kernel(tc, q, k, v, out):
 
         k_rows = keep.tile([P, KVH, PACK, D], BF16)
         v_rows = keep.tile([P, KVH, PACK, D], BF16)
-        q_rows = keep.tile([P, H, QT, D], BF16)
+        q_rows = keep.tile([P, KVH, QT, GROUP, D], BF16)
 
         def load_keys(rows, src, g):
             nc.sync.dma_start(out=rows[:, g], in_=src[0, g].rearrange("(p t) d -> p t d", t=PACK))
 
-        def load_queries(queue, h):
-            queue.dma_start(out=q_rows[:, h], in_=q[0, h].rearrange("(i r) d -> r i d", r=P))
+        def load_queries(g, m, first, end):
+            nc.sync.dma_start(
+                out=q_rows[:, g, first:end, m, :],
+                in_=q[0, g + KVH * m, first * P : end * P].rearrange("(i r) d -> r i d", r=P),
+            )
+
+        def load_query_tile(queue, i):
+            queue.dma_start(
+                out=q_rows[:, 0, i],
+                in_=q[0, 0::KVH, i * P : (i + 1) * P, :].rearrange("m r d -> r m d"),
+            )
 
         load_keys(k_rows, k, 0)
-        load_queries(nc.scalar, 0)
-        load_queries(nc.sync, KVH)
-        load_keys(v_rows, v, 0)
-        load_keys(v_rows, v, 1)
+        load_query_tile(nc.scalar, QT - 1)
+        load_query_tile(nc.sync, 0)
+        load_queries(0, 0, 1, QT - 1)
+        load_queries(0, 1, 1, QT - 1)
         load_keys(k_rows, k, 1)
-        load_queries(nc.sync, 1)
-        load_queries(nc.sync, 1 + KVH)
+        load_keys(v_rows, v, 0)
+        load_queries(1, 0, 0, QT)
+        load_queries(1, 1, 0, QT)
+        load_keys(v_rows, v, 1)
 
         zeros = keep.tile([P, N], BF16)
         nc.vector.memset(zeros[:].bitcast(F32), 0.0)
@@ -77,7 +116,7 @@ def tile_attend_s_kernel(tc, q, k, v, out):
             nc.tensor.matmul(out=idle_ps[:], lhsT=zeros[:, :P], rhs=zeros[:], start=True, stop=True)
         ident_bf = keep.tile([P, P], BF16)
         make_identity(nc, ident_bf[:])
-        causal = keep.tile([P, P], F32)
+        causal = keep.tile([P, BQ], F32)
         nc.gpsimd.memset(causal[:], 0.0)
         nc.gpsimd.affine_select(
             out=causal[:],
@@ -85,7 +124,7 @@ def tile_attend_s_kernel(tc, q, k, v, out):
             compare_op=ALU.is_ge,
             fill=MASKED,
             base=0,
-            pattern=[[-1, P]],
+            pattern=[[-1, BQ]],
             channel_multiplier=1,
         )
         ident_f32 = keep.tile([P, P], F32)
@@ -95,7 +134,7 @@ def tile_attend_s_kernel(tc, q, k, v, out):
         nc.scalar.activation(out=warm[:], in_=warm[:], func=ACT.Exp)
 
         kT = keep.tile([P, KVH, PAIRS, PAIR_COLS], BF16)
-        qT = keep.tile([P, H, QT, P], BF16)
+        qT = keep.tile([P, KVH, BANDS, GROUP, BQ], BF16)
         e_all = keep.tile([P, U, PAIRS, PAIR_COLS], BF16)
         row_max = keep.tile([P, U, 2], F32)
         shift = keep.tile([P, U, 2], F32)
@@ -105,21 +144,23 @@ def tile_attend_s_kernel(tc, q, k, v, out):
         e_codes = keep.tile([P, U, P], U32, align_bytes=64)
         e_scales = keep.tile([P, U, P], U8, align_bytes=64)
         v_grouped = keep.tile([P, KVH, D, PACK], BF16, align_bytes=64)
-        v_codes = keep.tile([P, KVH, D], U32, align_bytes=64)
-        v_scales = keep.tile([P, KVH, D], U8, align_bytes=64)
-        placed_codes = keep.tile([P, KVH, len(PLACES), D], U32, align_bytes=64)
-        placed_scales = keep.tile([P, KVH, len(PLACES), D], U8, align_bytes=64)
+        v_quant = keep.tile([P, KVH, ROW], U32, align_bytes=64)
+        v_copies = keep.tile([P, KVH, COPIES, ROW], U32, align_bytes=64)
         o_all = keep.tile([P, U, 2, D], F32)
 
-        nc.vector.memset(placed_codes[:].bitcast(I32), 0)
-        nc.vector.memset(placed_scales[:].bitcast(I32), 0)
-        nc.vector.memset(v_scales[:].bitcast(I32), 0)
+        nc.vector.memset(v_copies[:, 0].bitcast(I32), 0)
+        nc.vector.memset(v_quant[:, :, D:].bitcast(I32), 0)
         nc.vector.memset(row_sum[:], 1.0)
         causal_bf = keep.tile([P, PAIRS, STEP], BF16)
         nc.vector.tensor_copy(
-            out=causal_bf[:].rearrange("r u (p e) -> r u p e", e=2),
-            in_=causal[:].rearrange("r (p u e) -> r u p e", u=PAIRS, e=2),
+            out=causal_bf[:].rearrange("r u (w e) -> r u w e", e=2),
+            in_=causal[:].rearrange("r (w u e) -> r u w e", u=PAIRS, e=2),
         )
+        fold = keep.tile([P, GROUP, BQ], BF16)
+        nc.vector.tensor_copy(
+            out=fold[:], in_=ident_bf[:, :BQ].unsqueeze(1).to_broadcast([P, GROUP, BQ])
+        )
+        nc.gpsimd.memset(v_copies[:, 1].bitcast(I32), 0)
 
         def turn_keys(g, u, count):
             kt_ps = out_banks.tile([P, 2 * count, P], BF16, tag="o")
@@ -129,18 +170,34 @@ def tile_attend_s_kernel(tc, q, k, v, out):
 
         def keep_keys(kt_ps, g, u, count, copy):
             copy(
-                out=kT[:, g, u : u + count].rearrange("d u (p e) -> d u p e", e=2),
-                in_=kt_ps[:].rearrange("d (u e) p -> d u p e", e=2),
+                out=kT[:, g, u : u + count].rearrange("d u (w e) -> d u w e", e=2),
+                in_=kt_ps[:].rearrange("d (u e) w -> d u w e", e=2),
             )
 
-        def turn_queries(banks, tag, h, i, count):
-            qt_ps = banks.tile([P, count, P], BF16, tag=tag)
-            for c in range(count):
-                nc.tensor.transpose(qt_ps[:, c, :], q_rows[:, h, i + c, :], ident_bf[:])
+        def turn_queries(banks, tag, g, m, first, end):
+            qt_ps = banks.tile([P, end - first, P], BF16, tag=tag)
+            for i in range(first, end):
+                nc.tensor.transpose(qt_ps[:, i - first, :], q_rows[:, g, i, m, :], ident_bf[:])
             return qt_ps
 
-        def keep_queries(qt_ps, h, i, count, copy):
-            copy(out=qT[:, h, i : i + count], in_=qt_ps[:])
+        def keep_queries(qt_ps, g, m, first, end, copy):
+            copy(
+                out=qT[:, g, 2 * first : 2 * end, m, :],
+                in_=qt_ps[:].rearrange("d i (b c) -> d (i b) c", c=BQ),
+            )
+
+        def turn_tiles(tiles):
+            qt_ps = turn_banks.tile([P, len(tiles), GROUP, P], BF16, tag="turn")
+            for c, i in enumerate(tiles):
+                for m in range(GROUP):
+                    nc.tensor.transpose(qt_ps[:, c, m, :], q_rows[:, 0, i, m, :], ident_bf[:])
+            return qt_ps
+
+        def keep_tile(qt_ps, c, i, copy):
+            copy(
+                out=qT[:, 0, 2 * i : 2 * i + 2].rearrange("d b m c -> d m b c"),
+                in_=qt_ps[:, c].rearrange("d m (b c) -> d m b c", c=BQ),
+            )
 
         def group_values(g):
             nc.gpsimd.tensor_scalar(
@@ -152,66 +209,110 @@ def tile_attend_s_kernel(tc, q, k, v, out):
                 op1=ALU.add,
             )
 
+        def codes_of(row):
+            return row[:, :D].bitcast(FP8X4)
+
+        def scales_of(row):
+            return row[:, D:].bitcast(U8)
+
         def quantise_values(g):
+            row = v_quant[:, g, :]
             nc.vector.quantize_mx(
-                out=v_codes[:, g, :].bitcast(FP8X4),
-                scales=v_scales[:, g, :],
+                out=codes_of(row),
+                scales=scales_of(row),
                 in_=v_grouped[:, g].rearrange("p d t -> p (d t)"),
             )
-            for place, (i, base) in enumerate(PLACES):
-                rows = QUAD * (i + 1)
-                start = 0
-                for size in (2 * QUAD, QUAD):
-                    if rows - start >= size:
-                        nc.sync.dma_start(
-                            out=placed_codes[base + start : base + start + size, g, place, :].bitcast(I32),
-                            in_=v_codes[start : start + size, g, :].bitcast(I32),
-                        )
-                        nc.sync.dma_start(
-                            out=placed_scales[base + start : base + start + size, g, place, :].bitcast(I32),
-                            in_=v_scales[start : start + size, g, :].bitcast(I32),
-                        )
-                        start += size
+
+        def move(g, first, count, copies, to):
+            n_copies = copies.stop - copies.start
+            nc.sync.dma_start(
+                out=v_copies[to : to + count, g, copies, :].bitcast(I32),
+                in_=v_quant[first : first + count, g, :]
+                .bitcast(I32)
+                .unsqueeze(1)
+                .to_broadcast([count, n_copies, ROW]),
+            )
+
+        def move_scales(g, first, copy, to):
+            nc.sync.dma_start(
+                out=v_copies[to : to + 2, g, copy, D:].bitcast(I32),
+                in_=v_quant[first : first + 2, g, D:].bitcast(I32),
+            )
+
+        def place_pair(g, j):
+            if j == 0:
+                move(g, 0, BW, slice(LOW[0], LOW[0] + 1), P - BW)
+                move_scales(g, 0, LOW[0], P - 32 + 2)
+                move(g, 4 * BW, 2 * BW, slice(HIGH[6], HIGH[5] + 1), 4 * BW)
+                move(g, 6 * BW, BW, slice(HIGH[6], HIGH[6] + 1), 6 * BW)
+            if j == 1:
+                move(g, 0, 2 * BW, slice(LOW[1], LOW[2] + 1), P - 2 * BW)
+            if j == 2:
+                move(g, 4 * BW, BW, slice(HIGH[4], HIGH[4] + 1), 4 * BW)
+                move(g, 2 * BW, BW, slice(LOW[2], LOW[2] + 1), P - 3 * BW)
+                move_scales(g, 2 * BW, LOW[2], P // 2 + 2)
+
+        def place_values(g):
+            half = 4 * BW
+            if g == 0:
+                move(g, 0, half, slice(HIGH[6], HIGH[3] + 1), 0)
+                for j in (0, 1, 2):
+                    place_pair(g, j)
+            else:
+                move(g, 0, half, slice(HIGH[3], HIGH[3] + 1), half)
+                move(g, 0, half, slice(HIGH[6], HIGH[4] + 1), 0)
+                for j in (1, 2, 0):
+                    place_pair(g, j)
 
         s_tiles = {}
         et_tiles = {}
         o_tiles = {}
 
-        def columns(i, base):
-            return slice(2 * base, 2 * base + STEP * (i + 1))
-
-        def scores(n):
-            s_ps = score_banks.tile([P, PAIRS, PAIR_COLS], F32, tag="s")
-            for h, i, base in units[n]:
-                first = 2 * base
-                seen = STEP * i
-                diagonal = s_ps[:, :, first + seen : first + seen + STEP]
-                nc.tensor.matmul(out=diagonal, lhsT=ident_bf[:], rhs=causal_bf[:], start=True, stop=False)
+        def scores(n, bands):
+            if n not in s_tiles:
+                s_ps = score_banks.tile([P, PAIRS, PAIR_COLS], F32, tag="s")
+                s_tiles[n] = s_ps
+            s_ps = s_tiles[n]
+            for b in bands:
+                g, j, seen, own = UNITS[n][b]
+                band_q = qT[:, g, j].rearrange("d m c -> d (m c)")
+                diagonal = s_ps[:, :, 2 * own : 2 * own + STEP]
                 nc.tensor.matmul(
                     out=diagonal,
-                    lhsT=qT[:, h, i, :],
-                    rhs=kT[:, h % KVH, :, seen : seen + STEP],
+                    lhsT=fold[:].rearrange("c m i -> c (m i)"),
+                    rhs=causal_bf[:],
+                    start=True,
+                    stop=False,
+                )
+                nc.tensor.matmul(
+                    out=diagonal,
+                    lhsT=band_q,
+                    rhs=kT[:, g, :, STEP * j : STEP * (j + 1)],
                     start=False,
                     stop=True,
                 )
-                if seen > 0:
+                if j > 0:
                     nc.tensor.matmul(
-                        out=s_ps[:, :, first : first + seen],
-                        lhsT=qT[:, h, i, :],
-                        rhs=kT[:, h % KVH, :, :seen],
+                        out=s_ps[:, :, 2 * seen : 2 * seen + STEP * j],
+                        lhsT=band_q,
+                        rhs=kT[:, g, :, : STEP * j],
                         start=True,
                         stop=True,
                     )
-            s_tiles[n] = s_ps
 
-        def maxima(n):
-            for m, (h, i, base) in enumerate(units[n]):
+        def by_size(n):
+            return range(len(UNITS[n]) - 1, -1, -1)
+
+        def maxima(n, bands):
+            for b in bands:
                 nc.vector.reduce_max(
-                    out=row_max[:, n, m : m + 1], in_=s_tiles[n][:, :, columns(i, base)], axis=AXIS.XY
+                    out=row_max[:, n, b : b + 1],
+                    in_=s_tiles[n][:, :, columns(UNITS[n][b])],
+                    axis=AXIS.XY,
                 )
 
         def shifts(n):
-            members = len(units[n])
+            members = len(UNITS[n])
             if n == 0:
                 nc.scalar.mul(out=shift[:, n, :members], in_=row_max[:, n, :members], mul=-SCALE)
             else:
@@ -220,14 +321,15 @@ def tile_attend_s_kernel(tc, q, k, v, out):
                 )
 
         def exponentials(n):
-            for m, (h, i, base) in enumerate(units[n]):
+            for b in by_size(n):
+                cols = columns(UNITS[n][b])
                 nc.scalar.activation(
-                    out=e_all[:, n, :, columns(i, base)],
-                    in_=s_tiles[n][:, :, columns(i, base)],
+                    out=e_all[:, n, :, cols],
+                    in_=s_tiles[n][:, :, cols],
                     func=ACT.Exp,
-                    bias=shift[:, n, m : m + 1],
+                    bias=shift[:, n, b : b + 1],
                     scale=SCALE,
-                    accum_out=row_sum[:, n, m : m + 1],
+                    accum_out=row_sum[:, n, b : b + 1],
                 )
 
         def turn_e(n):
@@ -254,38 +356,49 @@ def tile_attend_s_kernel(tc, q, k, v, out):
 
         def multiply(n):
             o_ps = out_banks.tile([P, 2, D], F32, tag="o")
-            h, i, base = units[n][0]
-            g = h % KVH
-            if len(units[n]) == 1:
-                product = o_ps[:, 0, :]
-                values = v_codes[:, g, :]
-                value_scales = v_scales[:, g, :]
-            else:
-                place = PLACES.index((i, base))
-                product = o_ps[:].rearrange("r m d -> r (m d)")
-                values = placed_codes[:, g, place : place + 2, :].rearrange("p m d -> p (m d)")
-                value_scales = placed_scales[:, g, place : place + 2, :].rearrange("p m d -> p (m d)")
-            nc.tensor.matmul_mx(
-                out=product,
-                lhsT=e_codes[:, n, :].bitcast(FP8X4),
-                lhsT_scale=e_scales[:, n, :],
-                rhs=values.bitcast(FP8X4),
-                rhs_scale=value_scales,
-                start=True,
-                stop=True,
-            )
+            for b, (g, j, seen, own) in enumerate(UNITS[n]):
+                if len(UNITS[n]) == 1:
+                    row = v_quant[:, g, :]
+                elif j in LOW:
+                    row = v_copies[:, g, LOW[j], :]
+                else:
+                    row = v_copies[:, g, HIGH[j], :]
+                nc.tensor.matmul_mx(
+                    out=o_ps[:, b, :],
+                    lhsT=e_codes[:, n, :].bitcast(FP8X4),
+                    lhsT_scale=e_scales[:, n, :],
+                    rhs=codes_of(row),
+                    rhs_scale=scales_of(row),
+                    start=True,
+                    stop=True,
+                )
             o_tiles[n] = o_ps
 
         def finish(n):
-            members = len(units[n])
+            bands = UNITS[n]
+            members = len(bands)
             nc.vector.tensor_tensor(
                 out=o_all[:, n, :members, :],
                 in0=o_tiles[n][:, :members, :],
                 in1=inv_sum[:, n, :members].unsqueeze(2).to_broadcast([P, members, D]),
                 op=ALU.mult,
             )
-            for m, (h, i, base) in enumerate(units[n]):
-                nc.sync.dma_start(out=out[0, h, P * i : P * (i + 1), :], in_=o_all[:, n, m, :])
+            for m in range(GROUP):
+                rows = slice(BQ * m, BQ * (m + 1))
+                g, j = bands[0][:2]
+                if members == 1:
+                    nc.sync.dma_start(
+                        out=out[0, g + KVH * m, BQ * j : BQ * (j + 1), :], in_=o_all[rows, n, 0, :]
+                    )
+                elif bands[1][0] == g:
+                    other = bands[1][1]
+                    by_band = out[0, g + KVH * m].rearrange("(j c) d -> c j d", c=BQ)
+                    nc.sync.dma_start(
+                        out=by_band[:, j : other + 1 : other - j, :], in_=o_all[rows, n, :, :]
+                    )
+                else:
+                    by_head = out[0, KVH * m : KVH * (m + 1), BQ * j : BQ * (j + 1), :]
+                    nc.sync.dma_start(out=by_head.rearrange("g c d -> c g d"), in_=o_all[rows, n, :, :])
 
         def is_unit(n):
             return 0 <= n < U
@@ -294,46 +407,54 @@ def tile_attend_s_kernel(tc, q, k, v, out):
         keep_keys(first_k, 0, 0, 1, nc.vector.tensor_copy)
         second_k = turn_keys(0, 1, 1)
         keep_keys(second_k, 0, 1, 1, nc.scalar.copy)
-        first_q = turn_queries(turn_banks, "turn", 0, QT - 1, 1)
-        keep_queries(first_q, 0, QT - 1, 1, nc.vector.tensor_copy)
-        other_q = turn_queries(turn_banks, "turn", 0, 0, QT - 1)
-        keep_queries(other_q, 0, 0, QT - 1, nc.scalar.copy)
+        last_q = turn_tiles([QT - 1])
+        keep_tile(last_q, 0, QT - 1, nc.vector.tensor_copy)
+        first_q = turn_tiles([0])
+        keep_tile(first_q, 0, 0, nc.scalar.copy)
         turned = {}
-        turned["q"] = turn_queries(out_banks, "o", KVH, 0, QT)
-        keep_queries(turned["q"], KVH, 0, QT, nc.scalar.copy)
+        scores(0, by_size(0))
+        middle_q = turn_tiles([1, 2])
+        for c in range(2):
+            keep_tile(middle_q, c, c + 1, nc.scalar.copy)
+        scores(1, by_size(1))
+        maxima(0, by_size(0))
+        shifts(0)
+        maxima(1, by_size(1))
+        turned["k"] = turn_keys(1, 0, PAIRS)
+        scores(2, by_size(2))
         for g in range(KVH):
             group_values(g)
-        for n in range(-3, U + 3):
+        shifts(1)
+        quantise_values(0)
+        place_values(0)
+        turned["q"] = turn_queries(turn_banks, "turn", 1, 0, 0, QT)
+        for n in range(U + 3):
             if is_unit(n - 3):
                 multiply(n - 3)
             if is_unit(n + 3):
-                scores(n + 3)
-            if n == 0:
-                turned["q"] = turn_queries(out_banks, "o", 1, 0, QT)
-            if n == 1:
-                turned["q"] = turn_queries(out_banks, "o", 1 + KVH, 0, QT)
+                scores(n + 3, by_size(n + 3))
             if is_unit(n):
                 exponentials(n)
+                if n == 0:
+                    turned["later q"] = turn_queries(out_banks, "o", 1, 1, 0, QT)
                 turn_e(n)
             if is_unit(n + 2):
-                maxima(n + 2)
+                maxima(n + 2, by_size(n + 2))
                 shifts(n + 2)
+            if n == 0:
+                keep_queries(turned["q"], 1, 0, 0, QT, nc.vector.tensor_copy)
             if is_unit(n - 1):
                 regroup(n - 1)
-            if n == -2:
-                quantise_values(0)
-            if n == -1:
-                turned["k"] = turn_keys(1, 0, PAIRS)
+            if n == 0:
+                keep_keys(turned["k"], 1, 0, PAIRS, nc.scalar.copy)
+                keep_queries(turned["later q"], 1, 1, 0, QT, nc.vector.tensor_copy)
             if n == 0:
                 quantise_values(1)
-                keep_keys(turned["k"], 1, 0, PAIRS, nc.scalar.copy)
-                keep_queries(turned["q"], 1, 0, QT, nc.vector.tensor_copy)
-            if n == 1:
-                keep_queries(turned["q"], 1 + KVH, 0, QT, nc.vector.tensor_copy)
+                place_values(1)
             if n == 3:
                 invert(0, 1)
             if is_unit(n - 3) and (n - 3) % 3 == 1:
-                invert(n - 3, n)
+                invert(n - 3, min(n, U))
             if is_unit(n - 2):
                 quantise(n - 2)
             if is_unit(n - 3):

@@ -26,13 +26,12 @@ BW = BQ // PACK
 STEP = 2 * BW
 SCALE = D ** -0.5
 MASKED = -(2.0 ** 127)
-ROW = D + D // PACK
-
 FLOPS = 2 * 2 * H * N * N * D
 
 HIGH = {6: 0, 5: 1, 4: 2, 3: 3}
 LOW = {0: 4, 1: 5, 2: 6}
-COPIES = len(HIGH) + len(LOW)
+PLANES = len(HIGH) + len(LOW)
+LOW_CODES = {0: 0, 1: 1, 2: 1}
 
 
 def member(g, j, seen, own):
@@ -100,9 +99,8 @@ def tile_attend_s_kernel(tc, q, k, v, out):
 
         load_keys(k_rows, k, 0)
         load_query_tile(nc.scalar, QT - 1)
-        load_query_tile(nc.sync, 0)
-        load_queries(0, 0, 1, QT - 1)
-        load_queries(0, 1, 1, QT - 1)
+        load_queries(0, 0, 0, QT - 1)
+        load_queries(0, 1, 0, QT - 1)
         load_keys(k_rows, k, 1)
         load_keys(v_rows, v, 0)
         load_queries(1, 0, 0, QT)
@@ -144,12 +142,17 @@ def tile_attend_s_kernel(tc, q, k, v, out):
         e_codes = keep.tile([P, U, P], U32, align_bytes=64)
         e_scales = keep.tile([P, U, P], U8, align_bytes=64)
         v_grouped = keep.tile([P, KVH, D, PACK], BF16, align_bytes=64)
-        v_quant = keep.tile([P, KVH, ROW], U32, align_bytes=64)
-        v_copies = keep.tile([P, KVH, COPIES, ROW], U32, align_bytes=64)
-        o_all = keep.tile([P, U, 2, D], F32)
+        v_codes = keep.tile([P, KVH, D], U32, align_bytes=64)
+        v_scales = keep.tile([P, KVH, D], U8, align_bytes=64)
+        low_codes = keep.tile([P, KVH, 2, D], U32, align_bytes=64)
+        planes = keep.tile([P, KVH, PLANES, D], U8, align_bytes=64)
+        upper_codes = keep.tile([P, D], U32, align_bytes=64)
+        upper_scales = keep.tile([P, D], U8, align_bytes=64)
+        o_all = keep.tile([P, KVH, BANDS, D], F32)
 
-        nc.vector.memset(v_copies[:, 0].bitcast(I32), 0)
-        nc.vector.memset(v_quant[:, :, D:].bitcast(I32), 0)
+        nc.vector.memset(v_scales[:].bitcast(I32), 0)
+        nc.vector.memset(planes[:].bitcast(I32), 0)
+        nc.vector.memset(upper_scales[:].bitcast(I32), 0)
         nc.vector.memset(row_sum[:], 1.0)
         causal_bf = keep.tile([P, PAIRS, STEP], BF16)
         nc.vector.tensor_copy(
@@ -160,7 +163,8 @@ def tile_attend_s_kernel(tc, q, k, v, out):
         nc.vector.tensor_copy(
             out=fold[:], in_=ident_bf[:, :BQ].unsqueeze(1).to_broadcast([P, GROUP, BQ])
         )
-        nc.gpsimd.memset(v_copies[:, 1].bitcast(I32), 0)
+        nc.gpsimd.memset(low_codes[:].bitcast(I32), 0)
+        nc.gpsimd.memset(upper_codes[:].bitcast(I32), 0)
 
         def turn_keys(g, u, count):
             kt_ps = out_banks.tile([P, 2 * count, P], BF16, tag="o")
@@ -209,60 +213,35 @@ def tile_attend_s_kernel(tc, q, k, v, out):
                 op1=ALU.add,
             )
 
-        def codes_of(row):
-            return row[:, :D].bitcast(FP8X4)
-
-        def scales_of(row):
-            return row[:, D:].bitcast(U8)
-
         def quantise_values(g):
-            row = v_quant[:, g, :]
             nc.vector.quantize_mx(
-                out=codes_of(row),
-                scales=scales_of(row),
+                out=v_codes[:, g, :].bitcast(FP8X4),
+                scales=v_scales[:, g, :],
                 in_=v_grouped[:, g].rearrange("p d t -> p (d t)"),
             )
 
-        def move(g, first, count, copies, to):
-            n_copies = copies.stop - copies.start
-            nc.sync.dma_start(
-                out=v_copies[to : to + count, g, copies, :].bitcast(I32),
-                in_=v_quant[first : first + count, g, :]
-                .bitcast(I32)
-                .unsqueeze(1)
-                .to_broadcast([count, n_copies, ROW]),
-            )
-
-        def move_scales(g, first, copy, to):
-            nc.sync.dma_start(
-                out=v_copies[to : to + 2, g, copy, D:].bitcast(I32),
-                in_=v_quant[first : first + 2, g, D:].bitcast(I32),
-            )
-
-        def place_pair(g, j):
-            if j == 0:
-                move(g, 0, BW, slice(LOW[0], LOW[0] + 1), P - BW)
-                move_scales(g, 0, LOW[0], P - 32 + 2)
-                move(g, 4 * BW, 2 * BW, slice(HIGH[6], HIGH[5] + 1), 4 * BW)
-                move(g, 6 * BW, BW, slice(HIGH[6], HIGH[6] + 1), 6 * BW)
-            if j == 1:
-                move(g, 0, 2 * BW, slice(LOW[1], LOW[2] + 1), P - 2 * BW)
-            if j == 2:
-                move(g, 4 * BW, BW, slice(HIGH[4], HIGH[4] + 1), 4 * BW)
-                move(g, 2 * BW, BW, slice(LOW[2], LOW[2] + 1), P - 3 * BW)
-                move_scales(g, 2 * BW, LOW[2], P // 2 + 2)
+        def move(out, in_):
+            nc.sync.dma_start(out=out.bitcast(I32), in_=in_.bitcast(I32))
 
         def place_values(g):
-            half = 4 * BW
-            if g == 0:
-                move(g, 0, half, slice(HIGH[6], HIGH[3] + 1), 0)
-                for j in (0, 1, 2):
-                    place_pair(g, j)
-            else:
-                move(g, 0, half, slice(HIGH[3], HIGH[3] + 1), half)
-                move(g, 0, half, slice(HIGH[6], HIGH[4] + 1), 0)
-                for j in (1, 2, 0):
-                    place_pair(g, j)
+            for j, rows in ((6, 98), (5, 96), (4, 66), (3, 64)):
+                if j > 3 or g == 0:
+                    nc.gpsimd.tensor_copy(
+                        out=planes[:rows, g, HIGH[j], :].bitcast(U32),
+                        in_=v_scales[:rows, g, :].bitcast(U32),
+                    )
+            move(low_codes[P - BW :, g, 0, :], v_codes[:BW, g, :])
+            move(planes[P - 30 : P - 28, g, LOW[0], :], v_scales[:2, g, :])
+            move(low_codes[P - 2 * BW :, g, 1, :], v_codes[: 2 * BW, g, :])
+            move(
+                planes[P - 2 * BW : P - 2 * BW + 4, g, LOW[1] : LOW[2] + 1, :],
+                v_scales[:4, g, :].unsqueeze(1).to_broadcast([4, 2, D]),
+            )
+            move(low_codes[P - 3 * BW : P - 2 * BW, g, 1, :], v_codes[2 * BW : 3 * BW, g, :])
+            move(planes[P // 2 + 2 : P // 2 + 4, g, LOW[2], :], v_scales[2 * BW : 2 * BW + 2, g, :])
+            if g == 1:
+                move(upper_codes[P // 2 :, :], v_codes[: P // 2, g, :])
+                move(upper_scales[P // 2 :, :], v_scales[: P // 2, g, :])
 
         s_tiles = {}
         et_tiles = {}
@@ -313,7 +292,7 @@ def tile_attend_s_kernel(tc, q, k, v, out):
 
         def shifts(n):
             members = len(UNITS[n])
-            if n == 0:
+            if n < 2:
                 nc.scalar.mul(out=shift[:, n, :members], in_=row_max[:, n, :members], mul=-SCALE)
             else:
                 nc.gpsimd.tensor_scalar_mul(
@@ -357,48 +336,61 @@ def tile_attend_s_kernel(tc, q, k, v, out):
         def multiply(n):
             o_ps = out_banks.tile([P, 2, D], F32, tag="o")
             for b, (g, j, seen, own) in enumerate(UNITS[n]):
-                if len(UNITS[n]) == 1:
-                    row = v_quant[:, g, :]
-                elif j in LOW:
-                    row = v_copies[:, g, LOW[j], :]
-                else:
-                    row = v_copies[:, g, HIGH[j], :]
+                values, scales = v_codes[:, g, :], v_scales[:, g, :]
+                if j in LOW:
+                    values, scales = low_codes[:, g, LOW_CODES[j], :], planes[:, g, LOW[j], :]
+                elif j == 3 and g == 1:
+                    values, scales = upper_codes[:], upper_scales[:]
+                elif j in HIGH:
+                    scales = planes[:, g, HIGH[j], :]
                 nc.tensor.matmul_mx(
                     out=o_ps[:, b, :],
                     lhsT=e_codes[:, n, :].bitcast(FP8X4),
                     lhsT_scale=e_scales[:, n, :],
-                    rhs=codes_of(row),
-                    rhs_scale=scales_of(row),
+                    rhs=values.bitcast(FP8X4),
+                    rhs_scale=scales,
                     start=True,
                     stop=True,
                 )
             o_tiles[n] = o_ps
 
         def finish(n):
-            bands = UNITS[n]
-            members = len(bands)
+            g, j = UNITS[n][0][:2]
+            members = len(UNITS[n])
+            if members == 1:
+                target = o_all[:, g, j : j + 1, :]
+            elif UNITS[n][1][0] == g:
+                other = UNITS[n][1][1]
+                target = o_all[:, g, j : other + 1 : other - j, :]
+            else:
+                target = o_all[:, :, j, :]
             nc.vector.tensor_tensor(
-                out=o_all[:, n, :members, :],
+                out=target,
                 in0=o_tiles[n][:, :members, :],
                 in1=inv_sum[:, n, :members].unsqueeze(2).to_broadcast([P, members, D]),
                 op=ALU.mult,
             )
+
+        def store(g, first, last, step):
             for m in range(GROUP):
                 rows = slice(BQ * m, BQ * (m + 1))
-                g, j = bands[0][:2]
-                if members == 1:
-                    nc.sync.dma_start(
-                        out=out[0, g + KVH * m, BQ * j : BQ * (j + 1), :], in_=o_all[rows, n, 0, :]
-                    )
-                elif bands[1][0] == g:
-                    other = bands[1][1]
-                    by_band = out[0, g + KVH * m].rearrange("(j c) d -> c j d", c=BQ)
-                    nc.sync.dma_start(
-                        out=by_band[:, j : other + 1 : other - j, :], in_=o_all[rows, n, :, :]
-                    )
-                else:
-                    by_head = out[0, KVH * m : KVH * (m + 1), BQ * j : BQ * (j + 1), :]
-                    nc.sync.dma_start(out=by_head.rearrange("g c d -> c g d"), in_=o_all[rows, n, :, :])
+                bands = slice(first, last + 1, step)
+                nc.sync.dma_start(
+                    out=out[0, g + KVH * m].rearrange("(j c) d -> c j d", c=BQ)[:, bands, :],
+                    in_=o_all[rows, g, bands, :],
+                )
+
+        stores = [
+            (0, 7, 7, 1),
+            (0, 0, 6, 6),
+            (0, 1, 5, 4),
+            (0, 2, 4, 2),
+            (0, 3, 3, 1),
+            (1, 2, 4, 1),
+            (1, 1, 5, 4),
+            (1, 0, 6, 6),
+            (1, 7, 7, 1),
+        ]
 
         def is_unit(n):
             return 0 <= n < U
@@ -422,9 +414,7 @@ def tile_attend_s_kernel(tc, q, k, v, out):
         maxima(1, by_size(1))
         turned["k"] = turn_keys(1, 0, PAIRS)
         scores(2, by_size(2))
-        for g in range(KVH):
-            group_values(g)
-        shifts(1)
+        group_values(0)
         quantise_values(0)
         place_values(0)
         turned["q"] = turn_queries(turn_banks, "turn", 1, 0, 0, QT)
@@ -433,6 +423,8 @@ def tile_attend_s_kernel(tc, q, k, v, out):
                 multiply(n - 3)
             if is_unit(n + 3):
                 scores(n + 3, by_size(n + 3))
+            if n == 1:
+                shifts(1)
             if is_unit(n):
                 exponentials(n)
                 if n == 0:
@@ -449,6 +441,8 @@ def tile_attend_s_kernel(tc, q, k, v, out):
                 keep_keys(turned["k"], 1, 0, PAIRS, nc.scalar.copy)
                 keep_queries(turned["later q"], 1, 1, 0, QT, nc.vector.tensor_copy)
             if n == 0:
+                group_values(1)
+            if n == 1:
                 quantise_values(1)
                 place_values(1)
             if n == 3:
@@ -459,3 +453,4 @@ def tile_attend_s_kernel(tc, q, k, v, out):
                 quantise(n - 2)
             if is_unit(n - 3):
                 finish(n - 3)
+                store(*stores[n - 3])

@@ -16,7 +16,6 @@ AXIS = mybir.AxisListType
 P = 128
 H, KVH, N, D = 4, 2, 512, 128
 GROUP = H // KVH
-QT = N // P
 BQ = P // GROUP
 BANDS = N // BQ
 PACK = 4
@@ -62,6 +61,9 @@ UNITS = [
 ]
 
 
+TURNS = [[7, 6, 0, 5, 1, 4, 2, 3], [3, 2, 4, 1, 5, 0, 6, 7]]
+
+
 def columns(band):
     g, j, seen, own = band
     first = 2 * (own if j == 0 else min(seen, own))
@@ -80,31 +82,24 @@ def tile_attend_s_kernel(tc, q, k, v, out):
 
         k_rows = keep.tile([P, KVH, PACK, D], BF16)
         v_rows = keep.tile([P, KVH, PACK, D], BF16)
-        q_rows = keep.tile([P, KVH, QT, GROUP, D], BF16)
+        q_rows = keep.tile([P, KVH, BANDS, D], BF16)
 
         def load_keys(rows, src, g):
             nc.sync.dma_start(out=rows[:, g], in_=src[0, g].rearrange("(p t) d -> p t d", t=PACK))
 
-        def load_queries(g, m, first, end):
-            nc.sync.dma_start(
-                out=q_rows[:, g, first:end, m, :],
-                in_=q[0, g + KVH * m, first * P : end * P].rearrange("(i r) d -> r i d", r=P),
-            )
-
-        def load_query_tile(queue, i):
-            queue.dma_start(
-                out=q_rows[:, 0, i],
-                in_=q[0, 0::KVH, i * P : (i + 1) * P, :].rearrange("m r d -> r m d"),
-            )
+        def load_queries(queue, g, first, end):
+            for m in range(GROUP):
+                queue.dma_start(
+                    out=q_rows[m::GROUP, g, first:end, :],
+                    in_=q[0, g + KVH * m].rearrange("(j c) d -> c j d", c=BQ)[:, first:end, :],
+                )
 
         load_keys(k_rows, k, 0)
-        load_query_tile(nc.scalar, QT - 1)
-        load_queries(0, 0, 0, QT - 1)
-        load_queries(0, 1, 0, QT - 1)
+        load_queries(nc.scalar, 0, BANDS - 2, BANDS)
+        load_queries(nc.sync, 0, 0, BANDS - 2)
         load_keys(k_rows, k, 1)
         load_keys(v_rows, v, 0)
-        load_queries(1, 0, 0, QT)
-        load_queries(1, 1, 0, QT)
+        load_queries(nc.sync, 1, 0, BANDS)
         load_keys(v_rows, v, 1)
 
         zeros = keep.tile([P, N], BF16)
@@ -132,7 +127,7 @@ def tile_attend_s_kernel(tc, q, k, v, out):
         nc.scalar.activation(out=warm[:], in_=warm[:], func=ACT.Exp)
 
         kT = keep.tile([P, KVH, PAIRS, PAIR_COLS], BF16)
-        qT = keep.tile([P, KVH, BANDS, GROUP, BQ], BF16)
+        qT = keep.tile([P, KVH, BANDS, P], BF16)
         e_all = keep.tile([P, U, PAIRS, PAIR_COLS], BF16)
         row_max = keep.tile([P, U, 2], F32)
         shift = keep.tile([P, U, 2], F32)
@@ -159,9 +154,9 @@ def tile_attend_s_kernel(tc, q, k, v, out):
             out=causal_bf[:].rearrange("r u (w e) -> r u w e", e=2),
             in_=causal[:].rearrange("r (w u e) -> r u w e", u=PAIRS, e=2),
         )
-        fold = keep.tile([P, GROUP, BQ], BF16)
+        fold = keep.tile([P, BQ, GROUP], BF16)
         nc.vector.tensor_copy(
-            out=fold[:], in_=ident_bf[:, :BQ].unsqueeze(1).to_broadcast([P, GROUP, BQ])
+            out=fold[:], in_=ident_bf[:, :BQ].unsqueeze(2).to_broadcast([P, BQ, GROUP])
         )
         nc.gpsimd.memset(low_codes[:].bitcast(I32), 0)
         nc.gpsimd.memset(upper_codes[:].bitcast(I32), 0)
@@ -178,30 +173,16 @@ def tile_attend_s_kernel(tc, q, k, v, out):
                 in_=kt_ps[:].rearrange("d (u e) w -> d u w e", e=2),
             )
 
-        def turn_queries(banks, tag, g, m, first, end):
+        def turn_queries(banks, tag, g, first, end):
             qt_ps = banks.tile([P, end - first, P], BF16, tag=tag)
-            for i in range(first, end):
-                nc.tensor.transpose(qt_ps[:, i - first, :], q_rows[:, g, i, m, :], ident_bf[:])
+            for place in range(first, end):
+                nc.tensor.transpose(
+                    qt_ps[:, place - first, :], q_rows[:, g, TURNS[g][place], :], ident_bf[:]
+                )
             return qt_ps
 
-        def keep_queries(qt_ps, g, m, first, end, copy):
-            copy(
-                out=qT[:, g, 2 * first : 2 * end, m, :],
-                in_=qt_ps[:].rearrange("d i (b c) -> d (i b) c", c=BQ),
-            )
-
-        def turn_tiles(tiles):
-            qt_ps = turn_banks.tile([P, len(tiles), GROUP, P], BF16, tag="turn")
-            for c, i in enumerate(tiles):
-                for m in range(GROUP):
-                    nc.tensor.transpose(qt_ps[:, c, m, :], q_rows[:, 0, i, m, :], ident_bf[:])
-            return qt_ps
-
-        def keep_tile(qt_ps, c, i, copy):
-            copy(
-                out=qT[:, 0, 2 * i : 2 * i + 2].rearrange("d b m c -> d m b c"),
-                in_=qt_ps[:, c].rearrange("d m (b c) -> d m b c", c=BQ),
-            )
+        def keep_queries(qt_ps, g, first, end, copy):
+            copy(out=qT[:, g, first:end, :], in_=qt_ps[:])
 
         def group_values(g):
             nc.gpsimd.tensor_scalar(
@@ -254,11 +235,11 @@ def tile_attend_s_kernel(tc, q, k, v, out):
             s_ps = s_tiles[n]
             for b in bands:
                 g, j, seen, own = UNITS[n][b]
-                band_q = qT[:, g, j].rearrange("d m c -> d (m c)")
+                band_q = qT[:, g, TURNS[g].index(j), :]
                 diagonal = s_ps[:, :, 2 * own : 2 * own + STEP]
                 nc.tensor.matmul(
                     out=diagonal,
-                    lhsT=fold[:].rearrange("c m i -> c (m i)"),
+                    lhsT=fold[:].rearrange("c q m -> c (q m)"),
                     rhs=causal_bf[:],
                     start=True,
                     stop=False,
@@ -373,7 +354,7 @@ def tile_attend_s_kernel(tc, q, k, v, out):
 
         def store(g, first, last, step):
             for m in range(GROUP):
-                rows = slice(BQ * m, BQ * (m + 1))
+                rows = slice(m, P, GROUP)
                 bands = slice(first, last + 1, step)
                 nc.sync.dma_start(
                     out=out[0, g + KVH * m].rearrange("(j c) d -> c j d", c=BQ)[:, bands, :],
@@ -399,15 +380,14 @@ def tile_attend_s_kernel(tc, q, k, v, out):
         keep_keys(first_k, 0, 0, 1, nc.vector.tensor_copy)
         second_k = turn_keys(0, 1, 1)
         keep_keys(second_k, 0, 1, 1, nc.scalar.copy)
-        last_q = turn_tiles([QT - 1])
-        keep_tile(last_q, 0, QT - 1, nc.vector.tensor_copy)
-        first_q = turn_tiles([0])
-        keep_tile(first_q, 0, 0, nc.scalar.copy)
+        first_q = turn_queries(turn_banks, "turn", 0, 0, 1)
+        keep_queries(first_q, 0, 0, 1, nc.vector.tensor_copy)
+        second_q = turn_queries(turn_banks, "turn", 0, 1, 3)
+        keep_queries(second_q, 0, 1, 3, nc.scalar.copy)
         turned = {}
         scores(0, by_size(0))
-        middle_q = turn_tiles([1, 2])
-        for c in range(2):
-            keep_tile(middle_q, c, c + 1, nc.scalar.copy)
+        third_q = turn_queries(turn_banks, "turn", 0, 3, BANDS)
+        keep_queries(third_q, 0, 3, BANDS, nc.scalar.copy)
         scores(1, by_size(1))
         maxima(0, by_size(0))
         shifts(0)
@@ -417,7 +397,7 @@ def tile_attend_s_kernel(tc, q, k, v, out):
         group_values(0)
         quantise_values(0)
         place_values(0)
-        turned["q"] = turn_queries(turn_banks, "turn", 1, 0, 0, QT)
+        turned["q"] = turn_queries(turn_banks, "turn", 1, 0, 3)
         for n in range(U + 3):
             if is_unit(n - 3):
                 multiply(n - 3)
@@ -428,18 +408,18 @@ def tile_attend_s_kernel(tc, q, k, v, out):
             if is_unit(n):
                 exponentials(n)
                 if n == 0:
-                    turned["later q"] = turn_queries(out_banks, "o", 1, 1, 0, QT)
+                    turned["later q"] = turn_queries(out_banks, "o", 1, 3, BANDS)
                 turn_e(n)
             if is_unit(n + 2):
                 maxima(n + 2, by_size(n + 2))
                 shifts(n + 2)
             if n == 0:
-                keep_queries(turned["q"], 1, 0, 0, QT, nc.vector.tensor_copy)
+                keep_queries(turned["q"], 1, 0, 3, nc.vector.tensor_copy)
             if is_unit(n - 1):
                 regroup(n - 1)
             if n == 0:
                 keep_keys(turned["k"], 1, 0, PAIRS, nc.scalar.copy)
-                keep_queries(turned["later q"], 1, 1, 0, QT, nc.vector.tensor_copy)
+                keep_queries(turned["later q"], 1, 3, BANDS, nc.vector.tensor_copy)
             if n == 0:
                 group_values(1)
             if n == 1:

@@ -27,10 +27,8 @@ SCALE = D ** -0.5
 MASKED = -(2.0 ** 127)
 FLOPS = 2 * 2 * H * N * N * D
 
-HIGH = {6: 0, 5: 1, 4: 2, 3: 3}
-LOW = {0: 4, 1: 5, 2: 6}
-PLANES = len(HIGH) + len(LOW)
-LOW_CODES = {0: 0, 1: 1, 2: 1}
+LOW = (0, 1, 2)
+LOW_12, PLAIN, LOW_0 = 0, 1, 2
 
 
 def member(g, j, seen, own):
@@ -96,9 +94,9 @@ def tile_attend_s_kernel(tc, q, k, v, out):
 
         load_keys(k_rows, k, 0)
         load_queries(nc.scalar, 0, BANDS - 2, BANDS)
+        load_keys(v_rows, v, 0)
         load_queries(nc.sync, 0, 0, BANDS - 2)
         load_keys(k_rows, k, 1)
-        load_keys(v_rows, v, 0)
         load_queries(nc.sync, 1, 0, BANDS)
         load_keys(v_rows, v, 1)
 
@@ -137,10 +135,10 @@ def tile_attend_s_kernel(tc, q, k, v, out):
         e_codes = keep.tile([P, U, P], U32, align_bytes=64)
         e_scales = keep.tile([P, U, P], U8, align_bytes=64)
         v_grouped = keep.tile([P, KVH, D, PACK], BF16, align_bytes=64)
-        v_codes = keep.tile([P, KVH, D], U32, align_bytes=64)
+        v_codes = keep.tile([P, KVH, 3, D], U32, align_bytes=64)
         v_scales = keep.tile([P, KVH, D], U8, align_bytes=64)
-        low_codes = keep.tile([P, KVH, 2, D], U32, align_bytes=64)
-        planes = keep.tile([P, KVH, PLANES, D], U8, align_bytes=64)
+        planes = keep.tile([P, KVH, len(LOW), 2, D], U8, align_bytes=64)
+        lower_scales = keep.tile([P, D], U8, align_bytes=64)
         upper_codes = keep.tile([P, D], U32, align_bytes=64)
         upper_scales = keep.tile([P, D], U8, align_bytes=64)
         o_all = keep.tile([P, KVH, BANDS, D], F32)
@@ -148,6 +146,7 @@ def tile_attend_s_kernel(tc, q, k, v, out):
         nc.vector.memset(v_scales[:].bitcast(I32), 0)
         nc.vector.memset(planes[:].bitcast(I32), 0)
         nc.vector.memset(upper_scales[:].bitcast(I32), 0)
+        nc.vector.memset(lower_scales[:].bitcast(I32), 0)
         nc.vector.memset(row_sum[:], 1.0)
         causal_bf = keep.tile([P, PAIRS, STEP], BF16)
         nc.vector.tensor_copy(
@@ -158,7 +157,8 @@ def tile_attend_s_kernel(tc, q, k, v, out):
         nc.vector.tensor_copy(
             out=fold[:], in_=ident_bf[:, :BQ].unsqueeze(2).to_broadcast([P, BQ, GROUP])
         )
-        nc.gpsimd.memset(low_codes[:].bitcast(I32), 0)
+        for side in (LOW_12, LOW_0):
+            nc.gpsimd.memset(v_codes[:, :, side, :].bitcast(I32), 0)
         nc.gpsimd.memset(upper_codes[:].bitcast(I32), 0)
 
         def turn_keys(g, u, count):
@@ -196,7 +196,7 @@ def tile_attend_s_kernel(tc, q, k, v, out):
 
         def quantise_values(g):
             nc.vector.quantize_mx(
-                out=v_codes[:, g, :].bitcast(FP8X4),
+                out=v_codes[:, g, PLAIN, :].bitcast(FP8X4),
                 scales=v_scales[:, g, :],
                 in_=v_grouped[:, g].rearrange("p d t -> p (d t)"),
             )
@@ -204,61 +204,76 @@ def tile_attend_s_kernel(tc, q, k, v, out):
         def move(out, in_):
             nc.sync.dma_start(out=out.bitcast(I32), in_=in_.bitcast(I32))
 
+        def low_side(j):
+            return 1 if j == 0 else 0
+
         def place_values(g):
-            for j, rows in ((6, 98), (5, 96), (4, 66), (3, 64)):
-                if j > 3 or g == 0:
-                    nc.gpsimd.tensor_copy(
-                        out=planes[:rows, g, HIGH[j], :].bitcast(U32),
-                        in_=v_scales[:rows, g, :].bitcast(U32),
-                    )
-            move(low_codes[P - BW :, g, 0, :], v_codes[:BW, g, :])
-            move(planes[P - 30 : P - 28, g, LOW[0], :], v_scales[:2, g, :])
-            move(low_codes[P - 2 * BW :, g, 1, :], v_codes[: 2 * BW, g, :])
+            for j, rows in ((0, 98), (1, 96), (2, 66)):
+                nc.gpsimd.tensor_copy(
+                    out=planes[:rows, g, j, 1 - low_side(j), :].bitcast(U32),
+                    in_=v_scales[:rows, g, :].bitcast(U32),
+                )
+            if g == 0:
+                nc.gpsimd.tensor_copy(
+                    out=lower_scales[: P // 2, :].bitcast(U32), in_=v_scales[: P // 2, g, :].bitcast(U32)
+                )
+            plain = v_codes[:, g, PLAIN, :]
+            move(v_codes[P - BW :, g, LOW_0, :], plain[:BW, :])
+            move(planes[P - 30 : P - 28, g, 0, low_side(0), :], v_scales[:2, g, :])
+            move(v_codes[P - 2 * BW :, g, LOW_12, :], plain[: 2 * BW, :])
             move(
-                planes[P - 2 * BW : P - 2 * BW + 4, g, LOW[1] : LOW[2] + 1, :],
+                planes[P - 2 * BW : P - 2 * BW + 4, g, 1:3, low_side(1), :],
                 v_scales[:4, g, :].unsqueeze(1).to_broadcast([4, 2, D]),
             )
-            move(low_codes[P - 3 * BW : P - 2 * BW, g, 1, :], v_codes[2 * BW : 3 * BW, g, :])
-            move(planes[P // 2 + 2 : P // 2 + 4, g, LOW[2], :], v_scales[2 * BW : 2 * BW + 2, g, :])
+            move(v_codes[P - 3 * BW : P - 2 * BW, g, LOW_12, :], plain[2 * BW : 3 * BW, :])
+            move(planes[P // 2 + 2 : P // 2 + 4, g, 2, low_side(2), :], v_scales[2 * BW : 2 * BW + 2, g, :])
             if g == 1:
-                move(upper_codes[P // 2 :, :], v_codes[: P // 2, g, :])
+                move(upper_codes[P // 2 :, :], plain[: P // 2, :])
                 move(upper_scales[P // 2 :, :], v_scales[: P // 2, g, :])
 
         s_tiles = {}
         et_tiles = {}
         o_tiles = {}
 
-        def scores(n, bands):
-            if n not in s_tiles:
-                s_ps = score_banks.tile([P, PAIRS, PAIR_COLS], F32, tag="s")
-                s_tiles[n] = s_ps
-            s_ps = s_tiles[n]
-            for b in bands:
-                g, j, seen, own = UNITS[n][b]
-                band_q = qT[:, g, TURNS[g].index(j), :]
-                diagonal = s_ps[:, :, 2 * own : 2 * own + STEP]
+        def scores(n):
+            s_ps = score_banks.tile([P, PAIRS, PAIR_COLS], F32, tag="s")
+            if n == 0:
+                g, j, seen, own = UNITS[n][0]
+                own_cols = s_ps[:, :, 2 * own : 2 * own + STEP]
                 nc.tensor.matmul(
-                    out=diagonal,
-                    lhsT=fold[:].rearrange("c q m -> c (q m)"),
-                    rhs=causal_bf[:],
-                    start=True,
-                    stop=False,
+                    out=own_cols, lhsT=fold[:].rearrange("c q m -> c (q m)"), rhs=causal_bf[:], start=True, stop=False
                 )
                 nc.tensor.matmul(
-                    out=diagonal,
-                    lhsT=band_q,
-                    rhs=kT[:, g, :, STEP * j : STEP * (j + 1)],
+                    out=own_cols, lhsT=qT[:, g, 0, :], rhs=kT[:, g, :, STEP * j : STEP * (j + 1)], start=False, stop=True
+                )
+                nc.tensor.matmul(
+                    out=s_ps[:, :, : 2 * own], lhsT=qT[:, g, 0, :], rhs=kT[:, g, :, : STEP * j], start=True, stop=True
+                )
+                s_tiles[n] = s_ps
+                return
+            for b in by_size(n):
+                g, j, seen, own = UNITS[n][b]
+                cols = columns(UNITS[n][b])
+                own_cols = slice(2 * own, 2 * own + STEP)
+                runs = [(cols, 0)]
+                if own < seen:
+                    runs = [(slice(2 * seen, 2 * seen + STEP * j), 0), (own_cols, j)]
+                for run, first in runs:
+                    nc.tensor.matmul(
+                        out=s_ps[:, :, run],
+                        lhsT=qT[:, g, TURNS[g].index(j), :],
+                        rhs=kT[:, g, :, STEP * first : STEP * first + run.stop - run.start],
+                        start=True,
+                        stop=run is not runs[-1][0],
+                    )
+                nc.tensor.matmul(
+                    out=s_ps[:, :, own_cols],
+                    lhsT=fold[:].rearrange("c q m -> c (q m)"),
+                    rhs=causal_bf[:],
                     start=False,
                     stop=True,
                 )
-                if j > 0:
-                    nc.tensor.matmul(
-                        out=s_ps[:, :, 2 * seen : 2 * seen + STEP * j],
-                        lhsT=band_q,
-                        rhs=kT[:, g, :, : STEP * j],
-                        start=True,
-                        stop=True,
-                    )
+            s_tiles[n] = s_ps
 
         def by_size(n):
             return range(len(UNITS[n]) - 1, -1, -1)
@@ -316,16 +331,10 @@ def tile_attend_s_kernel(tc, q, k, v, out):
 
         def multiply(n):
             o_ps = out_banks.tile([P, 2, D], F32, tag="o")
-            for b, (g, j, seen, own) in enumerate(UNITS[n]):
-                values, scales = v_codes[:, g, :], v_scales[:, g, :]
-                if j in LOW:
-                    values, scales = low_codes[:, g, LOW_CODES[j], :], planes[:, g, LOW[j], :]
-                elif j == 3 and g == 1:
-                    values, scales = upper_codes[:], upper_scales[:]
-                elif j in HIGH:
-                    scales = planes[:, g, HIGH[j], :]
+
+            def product(out, values, scales):
                 nc.tensor.matmul_mx(
-                    out=o_ps[:, b, :],
+                    out=out,
                     lhsT=e_codes[:, n, :].bitcast(FP8X4),
                     lhsT_scale=e_scales[:, n, :],
                     rhs=values.bitcast(FP8X4),
@@ -333,6 +342,20 @@ def tile_attend_s_kernel(tc, q, k, v, out):
                     start=True,
                     stop=True,
                 )
+
+            g, j = UNITS[n][0][:2]
+            if len(UNITS[n]) == 1:
+                product(o_ps[:, 0, :], v_codes[:, g, PLAIN, :], v_scales[:, g, :])
+            elif j in LOW:
+                first = PLAIN if low_side(j) else LOW_12
+                product(
+                    o_ps[:].rearrange("r b d -> r (b d)"),
+                    v_codes[:, g, first : first + 2, :].rearrange("p s d -> p (s d)"),
+                    planes[:, g, j].rearrange("p s d -> p (s d)"),
+                )
+            else:
+                product(o_ps[:, 0, :], v_codes[:, 0, PLAIN, :], lower_scales[:])
+                product(o_ps[:, 1, :], upper_codes[:], upper_scales[:])
             o_tiles[n] = o_ps
 
         def finish(n):
@@ -345,9 +368,12 @@ def tile_attend_s_kernel(tc, q, k, v, out):
                 target = o_all[:, g, j : other + 1 : other - j, :]
             else:
                 target = o_all[:, :, j, :]
+            products = o_tiles[n][:, :members, :]
+            if members == 2 and low_side(j):
+                products = products[:, ::-1, :]
             nc.vector.tensor_tensor(
                 out=target,
-                in0=o_tiles[n][:, :members, :],
+                in0=products,
                 in1=inv_sum[:, n, :members].unsqueeze(2).to_broadcast([P, members, D]),
                 op=ALU.mult,
             )
@@ -385,24 +411,24 @@ def tile_attend_s_kernel(tc, q, k, v, out):
         second_q = turn_queries(turn_banks, "turn", 0, 1, 3)
         keep_queries(second_q, 0, 1, 3, nc.scalar.copy)
         turned = {}
-        scores(0, by_size(0))
+        scores(0)
         third_q = turn_queries(turn_banks, "turn", 0, 3, BANDS)
         keep_queries(third_q, 0, 3, BANDS, nc.scalar.copy)
-        scores(1, by_size(1))
+        scores(1)
+        group_values(0)
         maxima(0, by_size(0))
         shifts(0)
-        maxima(1, by_size(1))
-        turned["k"] = turn_keys(1, 0, PAIRS)
-        scores(2, by_size(2))
-        group_values(0)
         quantise_values(0)
         place_values(0)
+        maxima(1, by_size(1))
+        turned["k"] = turn_keys(1, 0, PAIRS)
+        scores(2)
         turned["q"] = turn_queries(turn_banks, "turn", 1, 0, 3)
         for n in range(U + 3):
+            if is_unit(n + 3):
+                scores(n + 3)
             if is_unit(n - 3):
                 multiply(n - 3)
-            if is_unit(n + 3):
-                scores(n + 3, by_size(n + 3))
             if n == 1:
                 shifts(1)
             if is_unit(n):

@@ -18,6 +18,7 @@ H, KVH, N, D = 4, 2, 512, 128
 GROUP = H // KVH
 BQ = P // GROUP
 BANDS = N // BQ
+NEAR = 2
 PACK = 4
 PAIRS = PACK // 2
 PAIR_COLS = N // PAIRS
@@ -59,9 +60,6 @@ UNITS = [
 ]
 
 
-TURNS = [[7, 6, 0, 5, 1, 4, 2, 3], [3, 2, 4, 1, 5, 0, 6, 7]]
-
-
 def columns(band):
     g, j, seen, own = band
     first = 2 * (own if j == 0 else min(seen, own))
@@ -80,24 +78,25 @@ def tile_attend_s_kernel(tc, q, k, v, out):
 
         k_rows = keep.tile([P, KVH, PACK, D], BF16)
         v_rows = keep.tile([P, KVH, PACK, D], BF16)
-        q_rows = keep.tile([P, KVH, BANDS, D], BF16)
+        q_rows = keep.tile([P, KVH, BANDS // NEAR, NEAR, D], BF16)
 
         def load_keys(rows, src, g):
             nc.sync.dma_start(out=rows[:, g], in_=src[0, g].rearrange("(p t) d -> p t d", t=PACK))
 
         def load_queries(queue, g, first, end):
             for m in range(GROUP):
+                pairs = q[0, g + KVH * m].rearrange("(i c t) d -> c i (t d)", c=BQ, t=NEAR)
                 queue.dma_start(
-                    out=q_rows[m::GROUP, g, first:end, :],
-                    in_=q[0, g + KVH * m].rearrange("(j c) d -> c j d", c=BQ)[:, first:end, :],
+                    out=q_rows[m::GROUP, g, first:end].rearrange("r i t d -> r i (t d)"),
+                    in_=pairs[:, first:end, :],
                 )
 
         load_keys(k_rows, k, 0)
-        load_queries(nc.scalar, 0, BANDS - 2, BANDS)
+        load_queries(nc.scalar, 0, 3, 4)
         load_keys(v_rows, v, 0)
-        load_queries(nc.sync, 0, 0, BANDS - 2)
+        load_queries(nc.sync, 0, 0, 3)
         load_keys(k_rows, k, 1)
-        load_queries(nc.sync, 1, 0, BANDS)
+        load_queries(nc.sync, 1, 0, 4)
         load_keys(v_rows, v, 1)
 
         zeros = keep.tile([P, N], BF16)
@@ -173,16 +172,19 @@ def tile_attend_s_kernel(tc, q, k, v, out):
                 in_=kt_ps[:].rearrange("d (u e) w -> d u w e", e=2),
             )
 
-        def turn_queries(banks, tag, g, first, end):
-            qt_ps = banks.tile([P, end - first, P], BF16, tag=tag)
-            for place in range(first, end):
-                nc.tensor.transpose(
-                    qt_ps[:, place - first, :], q_rows[:, g, TURNS[g][place], :], ident_bf[:]
-                )
+        def turn_queries(banks, tag, g, pairs):
+            qt_ps = banks.tile([P, len(pairs), NEAR * P], BF16, tag=tag)
+            for place, i in enumerate(pairs):
+                in_order = qt_ps[:, place, :].rearrange("d (c t m) -> d t c m", t=NEAR, m=GROUP)
+                for t in range(NEAR):
+                    nc.tensor.transpose(in_order[:, t], q_rows[:, g, i, t, :], ident_bf[:])
             return qt_ps
 
-        def keep_queries(qt_ps, g, first, end, copy):
-            copy(out=qT[:, g, first:end, :], in_=qt_ps[:])
+        def keep_queries(qt_ps, g, first, band, end, copy):
+            copy(
+                out=qT[:, g, band:end, :],
+                in_=qt_ps[:].rearrange("d i (b r) -> d (i b) r", r=P)[:, band - first : end - first, :],
+            )
 
         def group_values(g):
             nc.gpsimd.tensor_scalar(
@@ -244,10 +246,10 @@ def tile_attend_s_kernel(tc, q, k, v, out):
                     out=own_cols, lhsT=fold[:].rearrange("c q m -> c (q m)"), rhs=causal_bf[:], start=True, stop=False
                 )
                 nc.tensor.matmul(
-                    out=own_cols, lhsT=qT[:, g, 0, :], rhs=kT[:, g, :, STEP * j : STEP * (j + 1)], start=False, stop=True
+                    out=own_cols, lhsT=qT[:, g, j, :], rhs=kT[:, g, :, STEP * j : STEP * (j + 1)], start=False, stop=True
                 )
                 nc.tensor.matmul(
-                    out=s_ps[:, :, : 2 * own], lhsT=qT[:, g, 0, :], rhs=kT[:, g, :, : STEP * j], start=True, stop=True
+                    out=s_ps[:, :, : 2 * own], lhsT=qT[:, g, j, :], rhs=kT[:, g, :, : STEP * j], start=True, stop=True
                 )
                 s_tiles[n] = s_ps
                 return
@@ -261,7 +263,7 @@ def tile_attend_s_kernel(tc, q, k, v, out):
                 for run, first in runs:
                     nc.tensor.matmul(
                         out=s_ps[:, :, run],
-                        lhsT=qT[:, g, TURNS[g].index(j), :],
+                        lhsT=qT[:, g, j, :],
                         rhs=kT[:, g, :, STEP * first : STEP * first + run.stop - run.start],
                         start=True,
                         stop=run is not runs[-1][0],
@@ -406,14 +408,15 @@ def tile_attend_s_kernel(tc, q, k, v, out):
         keep_keys(first_k, 0, 0, 1, nc.vector.tensor_copy)
         second_k = turn_keys(0, 1, 1)
         keep_keys(second_k, 0, 1, 1, nc.scalar.copy)
-        first_q = turn_queries(turn_banks, "turn", 0, 0, 1)
-        keep_queries(first_q, 0, 0, 1, nc.vector.tensor_copy)
-        second_q = turn_queries(turn_banks, "turn", 0, 1, 3)
-        keep_queries(second_q, 0, 1, 3, nc.scalar.copy)
+        last_q = turn_queries(turn_banks, "turn", 0, [3])
+        keep_queries(last_q, 0, 6, 7, 8, nc.vector.tensor_copy)
+        keep_queries(last_q, 0, 6, 6, 7, nc.scalar.copy)
+        first_q = turn_queries(turn_banks, "turn", 0, [0])
+        keep_queries(first_q, 0, 0, 0, 2, nc.scalar.copy)
         turned = {}
         scores(0)
-        third_q = turn_queries(turn_banks, "turn", 0, 3, BANDS)
-        keep_queries(third_q, 0, 3, BANDS, nc.scalar.copy)
+        middle_q = turn_queries(turn_banks, "turn", 0, [1, 2])
+        keep_queries(middle_q, 0, 2, 2, 6, nc.scalar.copy)
         scores(1)
         group_values(0)
         maxima(0, by_size(0))
@@ -421,9 +424,9 @@ def tile_attend_s_kernel(tc, q, k, v, out):
         quantise_values(0)
         place_values(0)
         maxima(1, by_size(1))
-        turned["k"] = turn_keys(1, 0, PAIRS)
         scores(2)
-        turned["q"] = turn_queries(turn_banks, "turn", 1, 0, 3)
+        turned["k"] = turn_keys(1, 0, PAIRS)
+        turned["q"] = turn_queries(turn_banks, "turn", 1, [1, 2])
         for n in range(U + 3):
             if is_unit(n + 3):
                 scores(n + 3)
@@ -433,21 +436,25 @@ def tile_attend_s_kernel(tc, q, k, v, out):
                 shifts(1)
             if is_unit(n):
                 exponentials(n)
-                if n == 0:
-                    turned["later q"] = turn_queries(out_banks, "o", 1, 3, BANDS)
                 turn_e(n)
+                if n == 0:
+                    turned["later q"] = turn_queries(out_banks, "o", 1, [0, 3])
             if is_unit(n + 2):
                 maxima(n + 2, by_size(n + 2))
                 shifts(n + 2)
             if n == 0:
-                keep_queries(turned["q"], 1, 0, 3, nc.vector.tensor_copy)
+                keep_queries(turned["q"], 1, 2, 2, 6, nc.vector.tensor_copy)
             if is_unit(n - 1):
                 regroup(n - 1)
             if n == 0:
                 keep_keys(turned["k"], 1, 0, PAIRS, nc.scalar.copy)
-                keep_queries(turned["later q"], 1, 3, BANDS, nc.vector.tensor_copy)
-            if n == 0:
                 group_values(1)
+            if n == 1:
+                for place, i in enumerate((0, 3)):
+                    nc.vector.tensor_copy(
+                        out=qT[:, 1, NEAR * i : NEAR * (i + 1), :],
+                        in_=turned["later q"][:, place, :].rearrange("d (b r) -> d b r", r=P),
+                    )
             if n == 1:
                 quantise_values(1)
                 place_values(1)

@@ -102,7 +102,7 @@ def tile_attend_s_kernel(tc, q, k, v, out):
         zeros = keep.tile([P, N], BF16)
         nc.vector.memset(zeros[:].bitcast(F32), 0.0)
         idle_ps = score_banks.tile([P, N], F32, tag="s")
-        for repeat in range(3):
+        for repeat in range(4):
             nc.tensor.matmul(out=idle_ps[:], lhsT=zeros[:, :P], rhs=zeros[:], start=True, stop=True)
         ident_bf = keep.tile([P, P], BF16)
         make_identity(nc, ident_bf[:])
@@ -281,6 +281,13 @@ def tile_attend_s_kernel(tc, q, k, v, out):
             return range(len(UNITS[n]) - 1, -1, -1)
 
         def maxima(n, bands):
+            if UNITS[n][0][1] == UNITS[n][-1][1] and len(bands) == 2:
+                nc.vector.reduce_max(
+                    out=row_max[:, n, :],
+                    in_=s_tiles[n][:].rearrange("r u (b c) -> r b u c", b=2),
+                    axis=AXIS.XY,
+                )
+                return
             for b in bands:
                 nc.vector.reduce_max(
                     out=row_max[:, n, b : b + 1],
@@ -412,11 +419,13 @@ def tile_attend_s_kernel(tc, q, k, v, out):
         keep_queries(last_q, 0, 6, 7, 8, nc.vector.tensor_copy)
         keep_queries(last_q, 0, 6, 6, 7, nc.scalar.copy)
         first_q = turn_queries(turn_banks, "turn", 0, [0])
-        keep_queries(first_q, 0, 0, 0, 2, nc.scalar.copy)
+        keep_queries(first_q, 0, 0, 0, 2, nc.vector.tensor_copy)
         turned = {}
         scores(0)
-        middle_q = turn_queries(turn_banks, "turn", 0, [1, 2])
-        keep_queries(middle_q, 0, 2, 2, 6, nc.scalar.copy)
+        third_q = turn_queries(turn_banks, "turn", 0, [2])
+        keep_queries(third_q, 0, 4, 4, 6, nc.scalar.copy)
+        second_q = turn_queries(out_banks, "o", 0, [1])
+        keep_queries(second_q, 0, 2, 2, 4, nc.scalar.copy)
         scores(1)
         group_values(0)
         maxima(0, by_size(0))
@@ -450,18 +459,15 @@ def tile_attend_s_kernel(tc, q, k, v, out):
                 keep_keys(turned["k"], 1, 0, PAIRS, nc.scalar.copy)
                 group_values(1)
             if n == 1:
-                for place, i in enumerate((0, 3)):
-                    nc.vector.tensor_copy(
-                        out=qT[:, 1, NEAR * i : NEAR * (i + 1), :],
-                        in_=turned["later q"][:, place, :].rearrange("d (b r) -> d b r", r=P),
-                    )
+                nc.vector.tensor_copy(
+                    out=qT[:, 1].rearrange("d (i b) r -> d i (b r)", b=NEAR)[:, ::3, :],
+                    in_=turned["later q"][:],
+                )
             if n == 1:
                 quantise_values(1)
                 place_values(1)
-            if n == 3:
-                invert(0, 1)
-            if is_unit(n - 3) and (n - 3) % 3 == 1:
-                invert(n - 3, min(n, U))
+            if is_unit(n - 3) and (n - 3) % 3 == 0:
+                invert(n - 3, n)
             if is_unit(n - 2):
                 quantise(n - 2)
             if is_unit(n - 3):

@@ -32,6 +32,9 @@ LOW = (0, 1, 2)
 LOW_12, PLAIN, LOW_0 = 0, 1, 2
 
 
+ON_SCALAR = (6,)
+
+
 def member(g, j, seen, own):
     return (g, j, seen, own)
 
@@ -83,20 +86,20 @@ def tile_attend_s_kernel(tc, q, k, v, out):
         def load_keys(rows, src, g):
             nc.sync.dma_start(out=rows[:, g], in_=src[0, g].rearrange("(p t) d -> p t d", t=PACK))
 
-        def load_queries(queue, g, first, end):
+        def load_queries(queue, g, wanted):
             for m in range(GROUP):
                 pairs = q[0, g + KVH * m].rearrange("(i c t) d -> c i (t d)", c=BQ, t=NEAR)
                 queue.dma_start(
-                    out=q_rows[m::GROUP, g, first:end].rearrange("r i t d -> r i (t d)"),
-                    in_=pairs[:, first:end, :],
+                    out=q_rows[m::GROUP, g, wanted].rearrange("r i t d -> r i (t d)"),
+                    in_=pairs[:, wanted, :],
                 )
 
         load_keys(k_rows, k, 0)
-        load_queries(nc.scalar, 0, 3, 4)
+        load_queries(nc.scalar, 0, slice(0, 4, 3))
         load_keys(v_rows, v, 0)
-        load_queries(nc.sync, 0, 0, 3)
+        load_queries(nc.sync, 0, slice(1, 3))
         load_keys(k_rows, k, 1)
-        load_queries(nc.sync, 1, 0, 4)
+        load_queries(nc.sync, 1, slice(0, 4))
         load_keys(v_rows, v, 1)
 
         zeros = keep.tile([P, N], BF16)
@@ -219,6 +222,8 @@ def tile_attend_s_kernel(tc, q, k, v, out):
                 nc.gpsimd.tensor_copy(
                     out=lower_scales[: P // 2, :].bitcast(U32), in_=v_scales[: P // 2, g, :].bitcast(U32)
                 )
+
+        def move_values(g):
             plain = v_codes[:, g, PLAIN, :]
             move(v_codes[P - BW :, g, LOW_0, :], plain[:BW, :])
             move(planes[P - 30 : P - 28, g, 0, low_side(0), :], v_scales[:2, g, :])
@@ -323,10 +328,8 @@ def tile_attend_s_kernel(tc, q, k, v, out):
                 nc.tensor.transpose(et_ps[:, u, :], e_words[:, u, :], ident_f32[:])
             et_tiles[n] = et_ps
 
-        def regroup(n):
-            nc.scalar.copy(
-                out=e_grouped[:, n].bitcast(F32), in_=et_tiles[n][:].rearrange("w u r -> w r u")
-            )
+        def regroup(n, copy):
+            copy(out=e_grouped[:, n].bitcast(F32), in_=et_tiles[n][:].rearrange("w u r -> w r u"))
 
         def invert(first, end):
             nc.vector.reciprocal(out=inv_sum[:, first:end, :], in_=row_sum[:, first:end, :])
@@ -380,12 +383,21 @@ def tile_attend_s_kernel(tc, q, k, v, out):
             products = o_tiles[n][:, :members, :]
             if members == 2 and low_side(j):
                 products = products[:, ::-1, :]
-            nc.vector.tensor_tensor(
-                out=target,
-                in0=products,
-                in1=inv_sum[:, n, :members].unsqueeze(2).to_broadcast([P, members, D]),
-                op=ALU.mult,
-            )
+            if n in ON_SCALAR:
+                for b in range(members):
+                    nc.scalar.activation(
+                        out=target[:, b, :],
+                        in_=products[:, b, :],
+                        func=ACT.Copy,
+                        scale=inv_sum[:, n, b : b + 1],
+                    )
+            else:
+                nc.vector.tensor_tensor(
+                    out=target,
+                    in0=products,
+                    in1=inv_sum[:, n, :members].unsqueeze(2).to_broadcast([P, members, D]),
+                    op=ALU.mult,
+                )
 
         def store(g, first, last, step):
             for m in range(GROUP):
@@ -432,6 +444,7 @@ def tile_attend_s_kernel(tc, q, k, v, out):
         shifts(0)
         quantise_values(0)
         place_values(0)
+        move_values(0)
         maxima(1, by_size(1))
         scores(2)
         turned["k"] = turn_keys(1, 0, PAIRS)
@@ -453,8 +466,8 @@ def tile_attend_s_kernel(tc, q, k, v, out):
                 shifts(n + 2)
             if n == 0:
                 keep_queries(turned["q"], 1, 2, 2, 6, nc.vector.tensor_copy)
-            if is_unit(n - 1):
-                regroup(n - 1)
+            if is_unit(n - 1) and n - 1 not in (8,):
+                regroup(n - 1, nc.scalar.copy)
             if n == 0:
                 keep_keys(turned["k"], 1, 0, PAIRS, nc.scalar.copy)
                 group_values(1)
@@ -463,13 +476,16 @@ def tile_attend_s_kernel(tc, q, k, v, out):
                     out=qT[:, 1].rearrange("d (i b) r -> d i (b r)", b=NEAR)[:, ::3, :],
                     in_=turned["later q"][:],
                 )
-            if n == 1:
+            if n == 2:
                 quantise_values(1)
+                move_values(1)
                 place_values(1)
             if is_unit(n - 3) and (n - 3) % 3 == 0:
                 invert(n - 3, n)
             if is_unit(n - 2):
                 quantise(n - 2)
+            if n - 1 in (8,):
+                regroup(n - 1, nc.vector.tensor_copy)
             if is_unit(n - 3):
                 finish(n - 3)
                 store(*stores[n - 3])

@@ -131,6 +131,7 @@ def tile_attend_s_kernel(tc, q, k, v, out):
         e_all = keep.tile([P, U, PAIRS, PAIR_COLS], BF16)
         row_max = keep.tile([P, U, 2], F32)
         shift = keep.tile([P, U, 2], F32)
+        shift_3 = keep.tile([P, 1, 2], F32)
         row_sum = keep.tile([P, U, 2], F32)
         inv_sum = keep.tile([P, U, 2], F32)
         e_grouped = keep.tile([P, U, P, PACK], BF16, align_bytes=64)
@@ -302,7 +303,11 @@ def tile_attend_s_kernel(tc, q, k, v, out):
 
         def shifts(n):
             members = len(UNITS[n])
-            if n < 2:
+            if n == 3:
+                nc.vector.tensor_scalar_mul(
+                    out=shift_3[:, 0, :members], in0=row_max[:, n, :members], scalar1=-SCALE
+                )
+            elif n < 2:
                 nc.scalar.mul(out=shift[:, n, :members], in_=row_max[:, n, :members], mul=-SCALE)
             else:
                 nc.gpsimd.tensor_scalar_mul(
@@ -316,7 +321,7 @@ def tile_attend_s_kernel(tc, q, k, v, out):
                     out=e_all[:, n, :, cols],
                     in_=s_tiles[n][:, :, cols],
                     func=ACT.Exp,
-                    bias=shift[:, n, b : b + 1],
+                    bias=shift_3[:, 0, b : b + 1] if n == 3 else shift[:, n, b : b + 1],
                     scale=SCALE,
                     accum_out=row_sum[:, n, b : b + 1],
                 )
@@ -342,7 +347,10 @@ def tile_attend_s_kernel(tc, q, k, v, out):
             )
 
         def multiply(n):
-            o_ps = out_banks.tile([P, 2, D], F32, tag="o")
+            if n < U - 1:
+                o_ps = out_banks.tile([P, 2, D], F32, tag="o")
+            else:
+                o_ps = score_banks.tile([P, 2, D], F32, tag="s")
 
             def product(out, values, scales):
                 nc.tensor.matmul_mx(
@@ -446,8 +454,8 @@ def tile_attend_s_kernel(tc, q, k, v, out):
         place_values(0)
         move_values(0)
         maxima(1, by_size(1))
-        scores(2)
         turned["k"] = turn_keys(1, 0, PAIRS)
+        scores(2)
         turned["q"] = turn_queries(turn_banks, "turn", 1, [1, 2])
         for n in range(U + 3):
             if is_unit(n + 3):
@@ -463,9 +471,11 @@ def tile_attend_s_kernel(tc, q, k, v, out):
                     turned["later q"] = turn_queries(out_banks, "o", 1, [0, 3])
             if is_unit(n + 2):
                 maxima(n + 2, by_size(n + 2))
-                shifts(n + 2)
+                if n > 1:
+                    shifts(n + 2)
             if n == 0:
                 keep_queries(turned["q"], 1, 2, 2, 6, nc.vector.tensor_copy)
+                shifts(2)
             if is_unit(n - 1) and n - 1 not in (8,):
                 regroup(n - 1, nc.scalar.copy)
             if n == 0:
@@ -476,6 +486,7 @@ def tile_attend_s_kernel(tc, q, k, v, out):
                     out=qT[:, 1].rearrange("d (i b) r -> d i (b r)", b=NEAR)[:, ::3, :],
                     in_=turned["later q"][:],
                 )
+                shifts(3)
             if n == 2:
                 quantise_values(1)
                 move_values(1)

from contextlib import ExitStack

import concourse.mybir as mybir
from concourse.masks import make_identity

F32 = mybir.dt.float32
BF16 = mybir.dt.bfloat16
U32 = mybir.dt.uint32
I32 = mybir.dt.int32
U8 = mybir.dt.uint8
FP8X4 = mybir.dt.float8_e4m3fn_x4
ALU = mybir.AluOpType
ACT = mybir.ActivationFunctionType
AXIS = mybir.AxisListType

P = 128
H, KVH, N, D = 4, 2, 512, 128
GROUP = H // KVH
BQ = P // GROUP
BANDS = N // BQ
NEAR = 2
PACK = 4
PAIRS = PACK // 2
PAIR_COLS = N // PAIRS
BW = BQ // PACK
STEP = 2 * BW
SCALE = D ** -0.5
MASKED = -(2.0 ** 127)
FLOPS = 2 * 2 * H * N * N * D

LOW = (0, 1, 2)
LOW_12, PLAIN, LOW_0 = 0, 1, 2


ON_SCALAR = (6,)


def member(g, j, seen, own):
    return (g, j, seen, own)


def high(g, j):
    return member(g, j, 0, BW * j)


LOW_PLACES = {0: (P - BW, P - BW), 1: (P - 2 * BW, P - BW), 2: (P - 2 * BW, P - 3 * BW)}


def low(g, j):
    return member(g, j, LOW_PLACES[j][0], LOW_PLACES[j][1])


UNITS = [
    [high(0, 7)],
    [low(0, 0), high(0, 6)],
    [low(0, 1), high(0, 5)],
    [low(0, 2), high(0, 4)],
    [high(0, 3), member(1, 3, P // 2, P // 2 + 3 * BW)],
    [low(1, 2), high(1, 4)],
    [low(1, 1), high(1, 5)],
    [low(1, 0), high(1, 6)],
    [high(1, 7)],
]


def columns(band):
    g, j, seen, own = band
    first = 2 * (own if j == 0 else min(seen, own))
    return slice(first, first + STEP * (j + 1))


def tile_attend_s_kernel(tc, q, k, v, out):
    nc = tc.nc
    U = len(UNITS)
    with ExitStack() as ctx:
        keep = ctx.enter_context(tc.tile_pool(name="keep", bufs=1))
        score_banks = ctx.enter_context(tc.psum_pool(name="score_banks", bufs=4))
        turn_banks = ctx.enter_context(tc.psum_pool(name="turn_banks", bufs=2))
        out_banks = ctx.enter_context(tc.psum_pool(name="out_banks", bufs=2))
        ctx.enter_context(tc.manual_schedule())

        k_rows = keep.tile([P, KVH, PACK, D], BF16)
        v_rows = keep.tile([P, KVH, PACK, D], BF16)
        q_rows = keep.tile([P, KVH, BANDS // NEAR, NEAR, D], BF16)

        def load_keys(rows, src, g):
            nc.sync.dma_start(out=rows[:, g], in_=src[0, g].rearrange("(p t) d -> p t d", t=PACK))

        def load_queries(queue, g, wanted):
            for m in range(GROUP):
                pairs = q[0, g + KVH * m].rearrange("(i c t) d -> c i (t d)", c=BQ, t=NEAR)
                queue.dma_start(
                    out=q_rows[m::GROUP, g, wanted].rearrange("r i t d -> r i (t d)"),
                    in_=pairs[:, wanted, :],
                )

        load_keys(k_rows, k, 0)
        load_queries(nc.scalar, 0, slice(0, 4, 3))
        load_keys(v_rows, v, 0)
        load_queries(nc.sync, 0, slice(1, 3))
        load_keys(k_rows, k, 1)
        load_queries(nc.sync, 1, slice(0, 4))
        load_keys(v_rows, v, 1)

        zeros = keep.tile([P, N], BF16)
        nc.vector.memset(zeros[:].bitcast(F32), 0.0)
        idle_ps = score_banks.tile([P, N], F32, tag="s")
        for repeat in range(4):
            nc.tensor.matmul(out=idle_ps[:], lhsT=zeros[:, :P], rhs=zeros[:], start=True, stop=True)
        ident_bf = keep.tile([P, P], BF16)
        make_identity(nc, ident_bf[:])
        causal = keep.tile([P, BQ], F32)
        nc.gpsimd.memset(causal[:], 0.0)
        nc.gpsimd.affine_select(
            out=causal[:],
            in_=causal[:],
            compare_op=ALU.is_ge,
            fill=MASKED,
            base=0,
            pattern=[[-1, BQ]],
            channel_multiplier=1,
        )
        ident_f32 = keep.tile([P, P], F32)
        make_identity(nc, ident_f32[:])
        warm = keep.tile([P, 1], F32)
        nc.vector.memset(warm[:], 0.0)
        nc.scalar.activation(out=warm[:], in_=warm[:], func=ACT.Exp)

        kT = keep.tile([P, KVH, PAIRS, PAIR_COLS], BF16)
        qT = keep.tile([P, KVH, BANDS, P], BF16)
        e_all = keep.tile([P, U, PAIRS, PAIR_COLS], BF16)
        row_max = keep.tile([P, U, 2], F32)
        shift = keep.tile([P, U, 2], F32)
        shift_3 = keep.tile([P, 1, 2], F32)
        row_sum = keep.tile([P, U, 2], F32)
        inv_sum = keep.tile([P, U, 2], F32)
        e_grouped = keep.tile([P, U, P, PACK], BF16, align_bytes=64)
        e_codes = keep.tile([P, U, P], U32, align_bytes=64)
        e_scales = keep.tile([P, U, P], U8, align_bytes=64)
        v_grouped = keep.tile([P, KVH, D, PACK], BF16, align_bytes=64)
        v_codes = keep.tile([P, KVH, 3, D], U32, align_bytes=64)
        v_scales = keep.tile([P, KVH, D], U8, align_bytes=64)
        planes = keep.tile([P, KVH, len(LOW), 2, D], U8, align_bytes=64)
        lower_scales = keep.tile([P, D], U8, align_bytes=64)
        upper_codes = keep.tile([P, D], U32, align_bytes=64)
        upper_scales = keep.tile([P, D], U8, align_bytes=64)
        o_all = keep.tile([P, KVH, BANDS, D], F32)

        nc.vector.memset(v_scales[:].bitcast(I32), 0)
        nc.vector.memset(planes[:].bitcast(I32), 0)
        nc.vector.memset(upper_scales[:].bitcast(I32), 0)
        nc.vector.memset(lower_scales[:].bitcast(I32), 0)
        nc.vector.memset(row_sum[:], 1.0)
        causal_bf = keep.tile([P, PAIRS, STEP], BF16)
        nc.vector.tensor_copy(
            out=causal_bf[:].rearrange("r u (w e) -> r u w e", e=2),
            in_=causal[:].rearrange("r (w u e) -> r u w e", u=PAIRS, e=2),
        )
        fold = keep.tile([P, BQ, GROUP], BF16)
        nc.vector.tensor_copy(
            out=fold[:], in_=ident_bf[:, :BQ].unsqueeze(2).to_broadcast([P, BQ, GROUP])
        )
        for side in (LOW_12, LOW_0):
            nc.gpsimd.memset(v_codes[:, :, side, :].bitcast(I32), 0)
        nc.gpsimd.memset(upper_codes[:].bitcast(I32), 0)

        def turn_keys(g, u, count):
            kt_ps = out_banks.tile([P, 2 * count, P], BF16, tag="o")
            for t in range(2 * count):
                nc.tensor.transpose(kt_ps[:, t, :], k_rows[:, g, 2 * u + t, :], ident_bf[:])
            return kt_ps

        def keep_keys(kt_ps, g, u, count, copy):
            copy(
                out=kT[:, g, u : u + count].rearrange("d u (w e) -> d u w e", e=2),
                in_=kt_ps[:].rearrange("d (u e) w -> d u w e", e=2),
            )

        def turn_queries(banks, tag, g, pairs):
            qt_ps = banks.tile([P, len(pairs), NEAR * P], BF16, tag=tag)
            for place, i in enumerate(pairs):
                in_order = qt_ps[:, place, :].rearrange("d (c t m) -> d t c m", t=NEAR, m=GROUP)
                for t in range(NEAR):
                    nc.tensor.transpose(in_order[:, t], q_rows[:, g, i, t, :], ident_bf[:])
            return qt_ps

        def keep_queries(qt_ps, g, first, band, end, copy):
            copy(
                out=qT[:, g, band:end, :],
                in_=qt_ps[:].rearrange("d i (b r) -> d (i b) r", r=P)[:, band - first : end - first, :],
            )

        def group_values(g):
            nc.gpsimd.tensor_scalar(
                out=v_grouped[:, g],
                in0=v_rows[:, g].rearrange("p t d -> p d t"),
                scalar1=1.0,
                scalar2=0.0,
                op0=ALU.mult,
                op1=ALU.add,
            )

        def quantise_values(g):
            nc.vector.quantize_mx(
                out=v_codes[:, g, PLAIN, :].bitcast(FP8X4),
                scales=v_scales[:, g, :],
                in_=v_grouped[:, g].rearrange("p d t -> p (d t)"),
            )

        def move(out, in_):
            nc.sync.dma_start(out=out.bitcast(I32), in_=in_.bitcast(I32))

        def low_side(j):
            return 1 if j == 0 else 0

        def place_values(g):
            for j, rows in ((0, 98), (1, 96), (2, 66)):
                nc.gpsimd.tensor_copy(
                    out=planes[:rows, g, j, 1 - low_side(j), :].bitcast(U32),
                    in_=v_scales[:rows, g, :].bitcast(U32),
                )
            if g == 0:
                nc.gpsimd.tensor_copy(
                    out=lower_scales[: P // 2, :].bitcast(U32), in_=v_scales[: P // 2, g, :].bitcast(U32)
                )

        def move_values(g):
            plain = v_codes[:, g, PLAIN, :]
            move(v_codes[P - BW :, g, LOW_0, :], plain[:BW, :])
            move(planes[P - 30 : P - 28, g, 0, low_side(0), :], v_scales[:2, g, :])
            move(v_codes[P - 2 * BW :, g, LOW_12, :], plain[: 2 * BW, :])
            move(
                planes[P - 2 * BW : P - 2 * BW + 4, g, 1:3, low_side(1), :],
                v_scales[:4, g, :].unsqueeze(1).to_broadcast([4, 2, D]),
            )
            move(v_codes[P - 3 * BW : P - 2 * BW, g, LOW_12, :], plain[2 * BW : 3 * BW, :])
            move(planes[P // 2 + 2 : P // 2 + 4, g, 2, low_side(2), :], v_scales[2 * BW : 2 * BW + 2, g, :])
            if g == 1:
                move(upper_codes[P // 2 :, :], plain[: P // 2, :])
                move(upper_scales[P // 2 :, :], v_scales[: P // 2, g, :])

        s_tiles = {}
        et_tiles = {}
        o_tiles = {}

        def scores(n):
            s_ps = score_banks.tile([P, PAIRS, PAIR_COLS], F32, tag="s")
            if n == 0:
                g, j, seen, own = UNITS[n][0]
                own_cols = s_ps[:, :, 2 * own : 2 * own + STEP]
                nc.tensor.matmul(
                    out=own_cols, lhsT=fold[:].rearrange("c q m -> c (q m)"), rhs=causal_bf[:], start=True, stop=False
                )
                nc.tensor.matmul(
                    out=own_cols, lhsT=qT[:, g, j, :], rhs=kT[:, g, :, STEP * j : STEP * (j + 1)], start=False, stop=True
                )
                nc.tensor.matmul(
                    out=s_ps[:, :, : 2 * own], lhsT=qT[:, g, j, :], rhs=kT[:, g, :, : STEP * j], start=True, stop=True
                )
                s_tiles[n] = s_ps
                return
            for b in by_size(n):
                g, j, seen, own = UNITS[n][b]
                cols = columns(UNITS[n][b])
                own_cols = slice(2 * own, 2 * own + STEP)
                runs = [(cols, 0)]
                if own < seen:
                    runs = [(slice(2 * seen, 2 * seen + STEP * j), 0), (own_cols, j)]
                for run, first in runs:
                    nc.tensor.matmul(
                        out=s_ps[:, :, run],
                        lhsT=qT[:, g, j, :],
                        rhs=kT[:, g, :, STEP * first : STEP * first + run.stop - run.start],
                        start=True,
                        stop=run is not runs[-1][0],
                    )
                nc.tensor.matmul(
                    out=s_ps[:, :, own_cols],
                    lhsT=fold[:].rearrange("c q m -> c (q m)"),
                    rhs=causal_bf[:],
                    start=False,
                    stop=True,
                )
            s_tiles[n] = s_ps

        def by_size(n):
            return range(len(UNITS[n]) - 1, -1, -1)

        def maxima(n, bands):
            if UNITS[n][0][1] == UNITS[n][-1][1] and len(bands) == 2:
                nc.vector.reduce_max(
                    out=row_max[:, n, :],
                    in_=s_tiles[n][:].rearrange("r u (b c) -> r b u c", b=2),
                    axis=AXIS.XY,
                )
                return
            for b in bands:
                nc.vector.reduce_max(
                    out=row_max[:, n, b : b + 1],
                    in_=s_tiles[n][:, :, columns(UNITS[n][b])],
                    axis=AXIS.XY,
                )

        def shifts(n):
            members = len(UNITS[n])
            if n == 3:
                nc.vector.tensor_scalar_mul(
                    out=shift_3[:, 0, :members], in0=row_max[:, n, :members], scalar1=-SCALE
                )
            elif n < 2:
                nc.scalar.mul(out=shift[:, n, :members], in_=row_max[:, n, :members], mul=-SCALE)
            else:
                nc.gpsimd.tensor_scalar_mul(
                    out=shift[:, n, :members], in0=row_max[:, n, :members], scalar1=-SCALE
                )

        def exponentials(n):
            for b in by_size(n):
                cols = columns(UNITS[n][b])
                nc.scalar.activation(
                    out=e_all[:, n, :, cols],
                    in_=s_tiles[n][:, :, cols],
                    func=ACT.Exp,
                    bias=shift_3[:, 0, b : b + 1] if n == 3 else shift[:, n, b : b + 1],
                    scale=SCALE,
                    accum_out=row_sum[:, n, b : b + 1],
                )

        def turn_e(n):
            et_ps = turn_banks.tile([P, PAIRS, P], F32, tag="turn")
            e_words = e_all[:, n].bitcast(F32)
            for u in range(PAIRS):
                nc.tensor.transpose(et_ps[:, u, :], e_words[:, u, :], ident_f32[:])
            et_tiles[n] = et_ps

        def regroup(n, copy):
            copy(out=e_grouped[:, n].bitcast(F32), in_=et_tiles[n][:].rearrange("w u r -> w r u"))

        def invert(first, end):
            nc.vector.reciprocal(out=inv_sum[:, first:end, :], in_=row_sum[:, first:end, :])

        def quantise(n):
            nc.vector.quantize_mx(
                out=e_codes[:, n, :].bitcast(FP8X4),
                scales=e_scales[:, n, :],
                in_=e_grouped[:, n].rearrange("w r t -> w (r t)"),
            )

        def multiply(n):
            if n < U - 1:
                o_ps = out_banks.tile([P, 2, D], F32, tag="o")
            else:
                o_ps = score_banks.tile([P, 2, D], F32, tag="s")

            def product(out, values, scales):
                nc.tensor.matmul_mx(
                    out=out,
                    lhsT=e_codes[:, n, :].bitcast(FP8X4),
                    lhsT_scale=e_scales[:, n, :],
                    rhs=values.bitcast(FP8X4),
                    rhs_scale=scales,
                    start=True,
                    stop=True,
                )

            g, j = UNITS[n][0][:2]
            if len(UNITS[n]) == 1:
                product(o_ps[:, 0, :], v_codes[:, g, PLAIN, :], v_scales[:, g, :])
            elif j in LOW:
                first = PLAIN if low_side(j) else LOW_12
                product(
                    o_ps[:].rearrange("r b d -> r (b d)"),
                    v_codes[:, g, first : first + 2, :].rearrange("p s d -> p (s d)"),
                    planes[:, g, j].rearrange("p s d -> p (s d)"),
                )
            else:
                product(o_ps[:, 0, :], v_codes[:, 0, PLAIN, :], lower_scales[:])
                product(o_ps[:, 1, :], upper_codes[:], upper_scales[:])
            o_tiles[n] = o_ps

        def finish(n):
            g, j = UNITS[n][0][:2]
            members = len(UNITS[n])
            if members == 1:
                target = o_all[:, g, j : j + 1, :]
            elif UNITS[n][1][0] == g:
                other = UNITS[n][1][1]
                target = o_all[:, g, j : other + 1 : other - j, :]
            else:
                target = o_all[:, :, j, :]
            products = o_tiles[n][:, :members, :]
            if members == 2 and low_side(j):
                products = products[:, ::-1, :]
            if n in ON_SCALAR:
                for b in range(members):
                    nc.scalar.activation(
                        out=target[:, b, :],
                        in_=products[:, b, :],
                        func=ACT.Copy,
                        scale=inv_sum[:, n, b : b + 1],
                    )
            else:
                nc.vector.tensor_tensor(
                    out=target,
                    in0=products,
                    in1=inv_sum[:, n, :members].unsqueeze(2).to_broadcast([P, members, D]),
                    op=ALU.mult,
                )

        def store(g, first, last, step):
            for m in range(GROUP):
                rows = slice(m, P, GROUP)
                bands = slice(first, last + 1, step)
                nc.sync.dma_start(
                    out=out[0, g + KVH * m].rearrange("(j c) d -> c j d", c=BQ)[:, bands, :],
                    in_=o_all[rows, g, bands, :],
                )

        stores = [
            (0, 7, 7, 1),
            (0, 0, 6, 6),
            (0, 1, 5, 4),
            (0, 2, 4, 2),
            (0, 3, 3, 1),
            (1, 2, 4, 1),
            (1, 1, 5, 4),
            (1, 0, 6, 6),
            (1, 7, 7, 1),
        ]

        def is_unit(n):
            return 0 <= n < U

        first_k = turn_keys(0, 0, 1)
        keep_keys(first_k, 0, 0, 1, nc.vector.tensor_copy)
        second_k = turn_keys(0, 1, 1)
        keep_keys(second_k, 0, 1, 1, nc.scalar.copy)
        last_q = turn_queries(turn_banks, "turn", 0, [3])
        keep_queries(last_q, 0, 6, 7, 8, nc.vector.tensor_copy)
        keep_queries(last_q, 0, 6, 6, 7, nc.scalar.copy)
        first_q = turn_queries(turn_banks, "turn", 0, [0])
        keep_queries(first_q, 0, 0, 0, 2, nc.vector.tensor_copy)
        turned = {}
        scores(0)
        third_q = turn_queries(turn_banks, "turn", 0, [2])
        keep_queries(third_q, 0, 4, 4, 6, nc.scalar.copy)
        second_q = turn_queries(out_banks, "o", 0, [1])
        keep_queries(second_q, 0, 2, 2, 4, nc.scalar.copy)
        scores(1)
        group_values(0)
        maxima(0, by_size(0))
        shifts(0)
        quantise_values(0)
        place_values(0)
        move_values(0)
        maxima(1, by_size(1))
        turned["k"] = turn_keys(1, 0, PAIRS)
        scores(2)
        turned["q"] = turn_queries(turn_banks, "turn", 1, [1, 2])
        for n in range(U + 3):
            if is_unit(n + 3):
                scores(n + 3)
            if is_unit(n - 3):
                multiply(n - 3)
            if n == 1:
                shifts(1)
            if is_unit(n):
                exponentials(n)
                turn_e(n)
                if n == 0:
                    turned["later q"] = turn_queries(out_banks, "o", 1, [0, 3])
            if is_unit(n + 2):
                maxima(n + 2, by_size(n + 2))
                if n > 1:
                    shifts(n + 2)
            if n == 0:
                keep_queries(turned["q"], 1, 2, 2, 6, nc.vector.tensor_copy)
                shifts(2)
            if is_unit(n - 1) and n - 1 not in (8,):
                regroup(n - 1, nc.scalar.copy)
            if n == 0:
                keep_keys(turned["k"], 1, 0, PAIRS, nc.scalar.copy)
                group_values(1)
            if n == 1:
                nc.vector.tensor_copy(
                    out=qT[:, 1].rearrange("d (i b) r -> d i (b r)", b=NEAR)[:, ::3, :],
                    in_=turned["later q"][:],
                )
                shifts(3)
            if n == 2:
                quantise_values(1)
                move_values(1)
                place_values(1)
            if is_unit(n - 3) and (n - 3) % 3 == 0:
                invert(n - 3, n)
            if is_unit(n - 2):
                quantise(n - 2)
            if n - 1 in (8,):
                regroup(n - 1, nc.vector.tensor_copy)
            if is_unit(n - 3):
                finish(n - 3)
                store(*stores[n - 3])
